import numpy as np
import ml_dtypes


def mxq(x, axis, fmt="e4m3"):
    dtype, down = {"e4m3": (ml_dtypes.float8_e4m3fn, 7), "e5m2": (ml_dtypes.float8_e5m2, 14)}[fmt]
    v = np.moveaxis(np.asarray(x, np.float32).astype(ml_dtypes.bfloat16).astype(np.float64), axis, -1)
    blocks = v.reshape(v.shape[:-1] + (-1, 32))
    amax = np.abs(blocks).max(-1, keepdims=True)
    byte = np.maximum(np.where(amax > 0, np.frexp(amax)[1] - 1 + 127, 0) - down, 1)
    scale = np.exp2(byte - 127.0)
    codes = (blocks / scale).astype(np.float32).astype(dtype).astype(np.float64)
    return np.moveaxis((codes * scale).reshape(v.shape), -1, axis)


WIDE = False


def mx_kscale(k):
    if not WIDE:
        return np.ones(k)
    levels = np.array([10, -10, 5, -5, 0])
    if k % 512:
        return np.exp2(np.random.permutation(np.resize(levels, k // 32))).repeat(32)
    a = np.empty((k // 512, 16))
    for p in range(k // 512):
        a[p, :8] = np.random.permutation(np.resize(levels, 8))
        for g in range(8):
            far = levels[np.abs(levels - a[p, g]) >= 10]
            a[p, g + 8] = far[np.random.randint(len(far))]
    return np.exp2(a.ravel()).repeat(32)


BF16 = ml_dtypes.bfloat16


def bf(x):
    return np.asarray(x, np.float32).astype(BF16)


def f64(x):
    return np.asarray(x).astype(np.float64)


NA, NB, ND, ED = 32, 32, 1024, 1024
K1 = 2 * ED


def setup_inputs():
    s, t = mx_kscale(K1), mx_kscale(ED)
    return {"edge_embeds": bf(np.random.standard_normal((NA, NB, K1)) * s),
            "a_proj": bf(np.random.standard_normal((NA, ED)) * 0.5 * t),
            "b_proj": bf(np.random.standard_normal((NB, ED)) * 0.5 * t),
            "We": bf(np.random.standard_normal((K1, ED)) * 0.7 / np.sqrt(K1) / s[:, None] * t),
            "be1": bf(np.random.standard_normal(ED) * 0.3 * t),
            "We2": bf(np.random.standard_normal((ED, ED)) * 0.5 / np.sqrt(ED) / t[:, None]),
            "be2": bf(np.random.standard_normal(ED) * 0.1)}


def reference(edge_embeds, a_proj, b_proj, We, be1, We2, be2):
    h = f64(a_proj)[:, None, :] + f64(b_proj)[None, :, :] + (mxq(f64(edge_embeds), 2, "e4m3") @ mxq(f64(We), 0, "e4m3")) + f64(be1)
    h = np.maximum(h, 0.0)
    edge_latent = np.maximum((mxq(h, 2, "e4m3") @ mxq(f64(We2), 0, "e4m3")) + f64(be2), 0.0)
    sum_a = edge_latent.sum(axis=1)
    sum_b = edge_latent.sum(axis=0)
    return edge_latent, sum_a, sum_b

@@ -1,0 +1,348 @@
+from contextlib import ExitStack
+
+import concourse.masks as masks
+import concourse.mybir as mybir
+
+F32 = mybir.dt.float32
+BF16 = mybir.dt.bfloat16
+U32 = mybir.dt.uint32
+U8 = mybir.dt.uint8
+FP8X4 = mybir.dt.float8_e4m3fn_x4
+ADD = mybir.AluOpType.add
+RELU = mybir.ActivationFunctionType.Relu
+AXIS_X = mybir.AxisListType.X
+
+P = 128
+PACK = 4
+K_PASS = P * PACK
+BANK = 512
+
+NA, NB = 32, 32
+ROWS = NA * NB
+K1 = 2048
+ED = 1024
+ROW_TILES = ROWS // P
+A_PER_TILE = P // NB
+PASSES_1 = K1 // K_PASS
+PASSES_2 = ED // K_PASS
+OUT_HALVES = ED // BANK
+OUT_TILES = ED // P
+
+FLOPS = 2 * ROWS * K1 * ED + 2 * ROWS * ED * ED
+
+
+def tile_bipartiteneuralmessagepassinglayer_pa_kernel(
+    tc, edge_embeds, a_proj, b_proj, We, be1, We2, be2, out_0, out_1, out_2
+):
+    nc = tc.nc
+    x_rows = edge_embeds.rearrange("a b k -> (a b) k")
+    latent_rows = out_0.rearrange("a b f -> (a b) f")
+
+    with ExitStack() as ctx:
+        keep = ctx.enter_context(tc.tile_pool(name="keep", bufs=1))
+        grouped_w = ctx.enter_context(tc.tile_pool(name="grouped_w", bufs=2))
+        grouped_x = ctx.enter_context(tc.tile_pool(name="grouped_x", bufs=2))
+        terms_pool = ctx.enter_context(tc.tile_pool(name="terms", bufs=3))
+        hidden = ctx.enter_context(tc.tile_pool(name="hidden", bufs=3))
+        latent_pool = ctx.enter_context(tc.tile_pool(name="latent", bufs=4))
+        psum_x = ctx.enter_context(tc.psum_pool(name="psum_x", bufs=2))
+        psum_plain = ctx.enter_context(tc.psum_pool(name="psum_plain", bufs=2))
+        psum_mx = ctx.enter_context(tc.psum_pool(name="psum_mx", bufs=4))
+        ctx.enter_context(tc.manual_schedule())
+
+        node_rows = keep.tile([P, ED], BF16)
+        nc.sync.dma_start(out=node_rows[0:NA, :], in_=a_proj)
+        nc.sync.dma_start(out=node_rows[NA : NA + NB, :], in_=b_proj)
+        nc.sync.dma_start(out=node_rows[NA + NB : P, :], in_=be1.partition_broadcast(P - NA - NB))
+
+        we_raw = keep.tile([P, OUT_HALVES, PASSES_1, PACK, BANK], BF16)
+        we2_raw = keep.tile([P, PASSES_2, PACK, ED], BF16)
+        x_raw = keep.tile([P, ROW_TILES * K1], BF16)
+        be2_all = keep.tile([P, ED], BF16)
+
+        def load_we_piece(half, c):
+            nc.sync.dma_start(
+                out=we_raw[:, half, c],
+                in_=We[
+                    c * K_PASS : (c + 1) * K_PASS, half * BANK : (half + 1) * BANK
+                ].rearrange("(p t) n -> p t n", t=PACK),
+            )
+
+        def load_x(rt):
+            nc.sync.dma_start(
+                out=x_raw[:, rt * K1 : (rt + 1) * K1], in_=x_rows[rt * P : (rt + 1) * P, :]
+            )
+
+        for c in range(PASSES_1):
+            load_we_piece(0, c)
+        load_x(0)
+        load_x(1)
+        for c in range(PASSES_1):
+            load_we_piece(1, c)
+            load_x(2 + c)
+        load_x(6)
+        load_x(7)
+        for g in range(PASSES_2):
+            nc.sync.dma_start(
+                out=we2_raw[:, g],
+                in_=We2[g * K_PASS : (g + 1) * K_PASS, :].rearrange("(p t) n -> p t n", t=PACK),
+            )
+        nc.sync.dma_start(out=be2_all[:], in_=be2.partition_broadcast(P))
+
+        ident = keep.tile([P, P], F32)
+        masks.make_identity(nc, ident[:])
+        table_warmer = keep.tile([P, 1], F32)
+        nc.scalar.activation(out=table_warmer[:], in_=ident[:, 0:1], func=RELU)
+
+        node_cols = keep.tile([P, ED], BF16)
+        nc.scalar.copy(
+            out=node_cols[:].rearrange("p (g s m) -> p g s m", g=PASSES_2, s=PACK),
+            in_=node_rows[:].rearrange("p (g m s) -> p g s m", g=PASSES_2, s=PACK),
+        )
+
+        pick = keep.tile([P, NA, NB], BF16)
+        nc.vector.tensor_tensor(
+            out=pick[:],
+            in0=ident[:, 0:NA].unsqueeze(2).to_broadcast([P, NA, NB]),
+            in1=ident[:, NA : NA + NB].unsqueeze(1).to_broadcast([P, NA, NB]),
+            op=ADD,
+        )
+        nc.vector.tensor_scalar_add(
+            out=pick[:], in0=pick[:], scalar1=ident[:, NA + NB : NA + NB + 1]
+        )
+        pick_cols = pick[:].rearrange("k i j -> k (i j)")
+
+        of_a_node = keep.tile([P, A_PER_TILE], F32)
+        nc.vector.tensor_reduce(
+            out=of_a_node[:],
+            in_=ident[:].rearrange("r (a j) -> r a j", a=A_PER_TILE),
+            axis=AXIS_X,
+            op=ADD,
+        )
+        of_b_node = keep.tile([P, NB], F32)
+        nc.vector.tensor_reduce(
+            out=of_b_node[:],
+            in_=ident[:].rearrange("r (a j) -> r j a", a=A_PER_TILE),
+            axis=AXIS_X,
+            op=ADD,
+        )
+        summers = keep.tile([P, ROW_TILES, P], F32)
+        nc.vector.memset(summers[:], 0.0)
+        for rt in range(ROW_TILES):
+            first_a = rt * A_PER_TILE
+            nc.vector.tensor_copy(
+                out=summers[:, rt, first_a : first_a + A_PER_TILE], in_=of_a_node[:]
+            )
+        nc.vector.tensor_copy(
+            out=summers[:, :, NA : NA + NB],
+            in_=of_b_node[:].unsqueeze(1).to_broadcast([P, ROW_TILES, NB]),
+        )
+
+        we_codes = keep.tile([P, PASSES_1 * ED], U32, align_bytes=64)
+        we_scales = keep.tile([P, PASSES_1 * ED], U8, align_bytes=64)
+        we2_codes = keep.tile([P, PASSES_2 * ED], U32, align_bytes=64)
+        we2_scales = keep.tile([P, PASSES_2 * ED], U8, align_bytes=64)
+        x_codes = keep.tile([P, ROW_TILES * PASSES_1 * P], U32, align_bytes=64)
+        x_scales = keep.tile([P, ROW_TILES * PASSES_1 * P], U8, align_bytes=64)
+        h_codes = keep.tile([P, ROW_TILES * PASSES_2 * P], U32, align_bytes=64)
+        h_scales = keep.tile([P, ROW_TILES * PASSES_2 * P], U8, align_bytes=64)
+
+        pieces = []
+        for half in range(OUT_HALVES):
+            for c in range(PASSES_1):
+                pieces.append((we_raw[:, half, c], we_codes, we_scales, c * ED + half * BANK))
+        for g in range(PASSES_2):
+            for half in range(OUT_HALVES):
+                cols = slice(half * BANK, (half + 1) * BANK)
+                pieces.append((we2_raw[:, g, :, cols], we2_codes, we2_scales, g * ED + half * BANK))
+        grouped_of = {}
+
+        def regroup_piece(index):
+            raw = pieces[index][0]
+            grouped = grouped_w.tile([P, BANK * PACK], BF16, align_bytes=64)
+            grouped_of[index] = grouped
+            if index < OUT_HALVES * PASSES_1:
+                by_column = grouped[:].rearrange("p (s m t) -> p s m t", s=PACK, t=PACK)
+                by_raw = raw.rearrange("p t (m s) -> p s m t", s=PACK)
+                nc.vector.tensor_copy(out=by_column[:, 0:2], in_=by_raw[:, 0:2])
+                nc.scalar.copy(out=by_column[:, 2:4], in_=by_raw[:, 2:4])
+                return
+            by_column = grouped[:].rearrange("p (n t) -> p n t", t=PACK)
+            first, second = slice(0, BANK // 2), slice(BANK // 2, BANK)
+            nc.vector.tensor_copy(
+                out=by_column[:, first, :].rearrange("p (n i) t -> p n t i", i=4),
+                in_=raw[:, :, first].rearrange("p t (n i) -> p n t i", i=4),
+            )
+            nc.scalar.copy(
+                out=by_column[:, second, :].rearrange("p (n i) t -> p n t i", i=4),
+                in_=raw[:, :, second].rearrange("p t (n i) -> p n t i", i=4),
+            )
+
+        def quantise_piece(index):
+            codes, scales, first_col = pieces[index][1:]
+            cols = slice(first_col, first_col + BANK)
+            nc.vector.quantize_mx(
+                out=codes[:, cols].bitcast(FP8X4),
+                scales=scales[:, cols],
+                in_=grouped_of[index][:],
+            )
+
+        x_words = x_raw[:].bitcast(F32)
+        words_per_row = K1 // 2
+
+        def transpose_x(rt):
+            grouped = grouped_x.tile([P, PASSES_1 * P * PACK], BF16, align_bytes=64)
+            grouped_words = grouped[:].bitcast(F32).rearrange(
+                "p (c r u) -> p c r u", c=PASSES_1, u=2
+            )
+            for pair in range(PASSES_1 // 2):
+                xt = psum_x.tile([P, 4, P], F32)
+                for quarter in range(4):
+                    c, u = divmod(pair * 4 + quarter, 2)
+                    first = rt * words_per_row + c * 2 * P
+                    nc.tensor.transpose(
+                        xt[:, quarter, :], x_words[:, first + u : first + 2 * P : 2], ident[:]
+                    )
+                nc.scalar.copy(
+                    out=grouped_words[:, 2 * pair : 2 * pair + 2, :, :],
+                    in_=xt[:].rearrange("p (c u) r -> p c r u", u=2),
+                )
+            return grouped
+
+        def quantise_x(rt, grouped):
+            cols = slice(rt * PASSES_1 * P, (rt + 1) * PASSES_1 * P)
+            nc.vector.quantize_mx(
+                out=x_codes[:, cols].bitcast(FP8X4), scales=x_scales[:, cols], in_=grouped[:]
+            )
+
+        def node_terms(rt, g):
+            terms_ps = psum_plain.tile([P, PACK, P], F32, tag="plain")
+            for t in range(PACK):
+                e_tile = g * PACK + t
+                nc.tensor.matmul(
+                    terms_ps[:, t, :],
+                    lhsT=node_cols[:, e_tile * P : (e_tile + 1) * P],
+                    rhs=pick_cols[:, rt * P : (rt + 1) * P],
+                    start=True,
+                    stop=True,
+                )
+            terms = terms_pool.tile([P, P, PACK], F32)
+            nc.scalar.copy(out=terms[:], in_=terms_ps[:].rearrange("p t r -> p r t"))
+            return terms
+
+        def first_product(rt, g, terms):
+            h_ps = psum_mx.tile([P, PACK, P], F32, tag="mx")
+            for t in range(PACK):
+                e_tile = g * PACK + t
+                for c in range(PASSES_1):
+                    w_cols = slice(c * ED + e_tile * P, c * ED + (e_tile + 1) * P)
+                    r_cols = slice((rt * PASSES_1 + c) * P, (rt * PASSES_1 + c + 1) * P)
+                    nc.tensor.matmul_mx(
+                        out=h_ps[:, t, :],
+                        lhsT=we_codes[:, w_cols].bitcast(FP8X4),
+                        lhsT_scale=we_scales[:, w_cols],
+                        rhs=x_codes[:, r_cols].bitcast(FP8X4),
+                        rhs_scale=x_scales[:, r_cols],
+                        start=(c == 0),
+                        stop=(c == PASSES_1 - 1),
+                    )
+            h_grouped = hidden.tile([P, P, PACK], BF16, align_bytes=64)
+            nc.vector.tensor_tensor(
+                out=h_grouped[:], in0=h_ps[:].rearrange("p t r -> p r t"), in1=terms[:], op=ADD
+            )
+            return h_grouped
+
+        def relu_hidden(h_grouped):
+            nc.vector.tensor_scalar_max(out=h_grouped[:], in0=h_grouped[:], scalar1=0.0)
+
+        def quantise_hidden(rt, g, h_grouped):
+            cols = slice((rt * PASSES_2 + g) * P, (rt * PASSES_2 + g + 1) * P)
+            nc.vector.quantize_mx(
+                out=h_codes[:, cols].bitcast(FP8X4),
+                scales=h_scales[:, cols],
+                in_=h_grouped[:].rearrange("p r t -> p (r t)"),
+            )
+
+        def second_product(rt):
+            latent = latent_pool.tile([P, ED], F32)
+            for half in range(OUT_HALVES):
+                o_ps = psum_mx.tile([P, BANK], F32, tag="mx")
+                for g in range(PASSES_2):
+                    r_cols = slice((rt * PASSES_2 + g) * P, (rt * PASSES_2 + g + 1) * P)
+                    f_cols = slice(g * ED + half * BANK, g * ED + (half + 1) * BANK)
+                    nc.tensor.matmul_mx(
+                        out=o_ps[:],
+                        lhsT=h_codes[:, r_cols].bitcast(FP8X4),
+                        lhsT_scale=h_scales[:, r_cols],
+                        rhs=we2_codes[:, f_cols].bitcast(FP8X4),
+                        rhs_scale=we2_scales[:, f_cols],
+                        start=(g == 0),
+                        stop=(g == PASSES_2 - 1),
+                    )
+                cols = slice(half * BANK, (half + 1) * BANK)
+                nc.vector.tensor_tensor(
+                    out=latent[:, cols], in0=o_ps[:], in1=be2_all[:, cols], op=ADD
+                )
+                nc.scalar.activation(out=latent[:, cols], in_=latent[:, cols], func=RELU)
+            nc.sync.dma_start(out=latent_rows[rt * P : (rt + 1) * P, :], in_=latent[:])
+            return latent
+
+        def add_to_sums(rt, latent, sums_ps):
+            for half in range(OUT_HALVES):
+                nc.tensor.matmul(
+                    sums_ps[half][:],
+                    lhsT=summers[:, rt, :],
+                    rhs=latent[:, half * BANK : (half + 1) * BANK],
+                    start=(rt == 0),
+                    stop=(rt == ROW_TILES - 1),
+                )
+
+        for index in range(PASSES_1):
+            regroup_piece(index)
+            if index > 0:
+                quantise_piece(index - 1)
+        quantise_piece(PASSES_1 - 1)
+
+        units = PASSES_2 * ROW_TILES
+        terms_of, h_of = {}, {}
+        for unit in range(-1, units + 1):
+            following, before = unit + 1, unit - 1
+            if following < units:
+                next_g, next_rt = divmod(following, ROW_TILES)
+                if next_g == 0:
+                    x_grouped = transpose_x(next_rt)
+                    quantise_x(next_rt, x_grouped)
+            if 0 <= unit < units:
+                g, rt = divmod(unit, ROW_TILES)
+                h_of[unit] = first_product(rt, g, terms_of[unit])
+            if following < units:
+                terms_of[following] = node_terms(next_rt, next_g)
+            if before >= 0:
+                relu_hidden(h_of[before])
+            if 0 <= unit < units:
+                index = PASSES_1 + unit // 2
+                if unit % 2 == 0:
+                    regroup_piece(index)
+                else:
+                    quantise_piece(index)
+            if before >= 0:
+                g, rt = divmod(before, ROW_TILES)
+                quantise_hidden(rt, g, h_of[before])
+
+        SUMS_BEHIND = 2
+        sums_ps = []
+        for half in range(OUT_HALVES):
+            half_ps = psum_plain.tile([P, BANK], F32, tag="plain")
+            sums_ps.append(half_ps)
+        latent_of = {}
+        for rt in range(ROW_TILES + SUMS_BEHIND):
+            if rt < ROW_TILES:
+                latent_of[rt] = second_product(rt)
+            if rt >= SUMS_BEHIND:
+                add_to_sums(rt - SUMS_BEHIND, latent_of[rt - SUMS_BEHIND], sums_ps)
+
+        sums = keep.tile([P, ED], F32)
+        nc.vector.tensor_copy(out=sums[:, 0:BANK], in_=sums_ps[0][:])
+        nc.scalar.copy(out=sums[:, BANK:ED], in_=sums_ps[1][:])
+        nc.sync.dma_start(out=out_1, in_=sums[0:NA, :])
+        nc.sync.dma_start(out=out_2, in_=sums[NA : NA + NB, :])

@@ -27,6 +27,10 @@ PASSES_1 = K1 // K_PASS
 PASSES_2 = ED // K_PASS
 OUT_HALVES = ED // BANK
 OUT_TILES = ED // P
+Q_ROWS = 2 * P
+QUARTERS = ROWS // Q_ROWS
+A_PER_QUARTER = Q_ROWS // NB
+BE1_ROW, BE2_ROW = 64, 96
 
 FLOPS = 2 * ROWS * K1 * ED + 2 * ROWS * ED * ED
 
@@ -40,25 +44,21 @@ def tile_bipartiteneuralmessagepassinglayer_pa_kernel(
 
     with ExitStack() as ctx:
         keep = ctx.enter_context(tc.tile_pool(name="keep", bufs=1))
-        grouped_w = ctx.enter_context(tc.tile_pool(name="grouped_w", bufs=2))
-        grouped_x = ctx.enter_context(tc.tile_pool(name="grouped_x", bufs=2))
-        terms_pool = ctx.enter_context(tc.tile_pool(name="terms", bufs=3))
+        grouped_w = ctx.enter_context(tc.tile_pool(name="grouped_w", bufs=3))
+        grouped_x = ctx.enter_context(tc.tile_pool(name="grouped_x", bufs=3))
+        terms_pool = ctx.enter_context(tc.tile_pool(name="terms", bufs=6))
         hidden = ctx.enter_context(tc.tile_pool(name="hidden", bufs=3))
         latent_pool = ctx.enter_context(tc.tile_pool(name="latent", bufs=4))
-        psum_x = ctx.enter_context(tc.psum_pool(name="psum_x", bufs=2))
+        trees = ctx.enter_context(tc.tile_pool(name="trees", bufs=2))
+        stores = ctx.enter_context(tc.tile_pool(name="stores", bufs=2))
+        psum_tr = ctx.enter_context(tc.psum_pool(name="psum_tr", bufs=2))
         psum_plain = ctx.enter_context(tc.psum_pool(name="psum_plain", bufs=2))
         psum_mx = ctx.enter_context(tc.psum_pool(name="psum_mx", bufs=4))
-        ctx.enter_context(tc.manual_schedule())
 
         node_rows = keep.tile([P, ED], BF16)
-        nc.sync.dma_start(out=node_rows[0:NA, :], in_=a_proj)
-        nc.sync.dma_start(out=node_rows[NA : NA + NB, :], in_=b_proj)
-        nc.sync.dma_start(out=node_rows[NA + NB : P, :], in_=be1.partition_broadcast(P - NA - NB))
-
         we_raw = keep.tile([P, OUT_HALVES, PASSES_1, PACK, BANK], BF16)
         we2_raw = keep.tile([P, PASSES_2, PACK, ED], BF16)
         x_raw = keep.tile([P, ROW_TILES * K1], BF16)
-        be2_all = keep.tile([P, ED], BF16)
 
         def load_we_piece(half, c):
             nc.sync.dma_start(
@@ -73,33 +73,44 @@ def tile_bipartiteneuralmessagepassinglayer_pa_kernel(
                 out=x_raw[:, rt * K1 : (rt + 1) * K1], in_=x_rows[rt * P : (rt + 1) * P, :]
             )
 
-        for c in range(PASSES_1):
-            load_we_piece(0, c)
+        load_we_piece(0, 0)
+        nc.sync.dma_start(out=node_rows[0:NA, :], in_=a_proj)
+        nc.sync.dma_start(out=node_rows[NA : NA + NB, :], in_=b_proj)
+        nc.sync.dma_start(out=node_rows[BE1_ROW:BE2_ROW, :], in_=be1.partition_broadcast(BE2_ROW - BE1_ROW))
+        nc.sync.dma_start(out=node_rows[BE2_ROW:P, :], in_=be2.partition_broadcast(P - BE2_ROW))
+        load_we_piece(0, 1)
         load_x(0)
+        load_we_piece(0, 2)
+        load_we_piece(0, 3)
         load_x(1)
-        for c in range(PASSES_1):
-            load_we_piece(1, c)
-            load_x(2 + c)
+        load_x(2)
+        load_x(3)
+        load_we_piece(1, 0)
+        load_we_piece(1, 1)
+        load_we_piece(1, 2)
+        load_we_piece(1, 3)
+        load_x(4)
+        nc.sync.dma_start(
+            out=we2_raw[:, 0],
+            in_=We2[0 * K_PASS : 1 * K_PASS, :].rearrange("(p t) n -> p t n", t=PACK),
+        )
+        nc.sync.dma_start(
+            out=we2_raw[:, 1],
+            in_=We2[1 * K_PASS : 2 * K_PASS, :].rearrange("(p t) n -> p t n", t=PACK),
+        )
+        load_x(5)
         load_x(6)
         load_x(7)
-        for g in range(PASSES_2):
-            nc.sync.dma_start(
-                out=we2_raw[:, g],
-                in_=We2[g * K_PASS : (g + 1) * K_PASS, :].rearrange("(p t) n -> p t n", t=PACK),
-            )
-        nc.sync.dma_start(out=be2_all[:], in_=be2.partition_broadcast(P))
 
+        sums_t = keep.tile([P, OUT_TILES, P], F32)
+        nc.vector.memset(sums_t[:], 0.0)
         ident = keep.tile([P, P], F32)
         masks.make_identity(nc, ident[:])
         table_warmer = keep.tile([P, 1], F32)
         nc.scalar.activation(out=table_warmer[:], in_=ident[:, 0:1], func=RELU)
 
-        node_cols = keep.tile([P, ED], BF16)
-        nc.scalar.copy(
-            out=node_cols[:].rearrange("p (g s m) -> p g s m", g=PASSES_2, s=PACK),
-            in_=node_rows[:].rearrange("p (g m s) -> p g s m", g=PASSES_2, s=PACK),
-        )
-
+        ident_bf = keep.tile([P, P], BF16)
+        nc.vector.tensor_copy(out=ident_bf[:], in_=ident[:])
         pick = keep.tile([P, NA, NB], BF16)
         nc.vector.tensor_tensor(
             out=pick[:],
@@ -111,31 +122,10 @@ def tile_bipartiteneuralmessagepassinglayer_pa_kernel(
             out=pick[:], in0=pick[:], scalar1=ident[:, NA + NB : NA + NB + 1]
         )
         pick_cols = pick[:].rearrange("k i j -> k (i j)")
-
-        of_a_node = keep.tile([P, A_PER_TILE], F32)
-        nc.vector.tensor_reduce(
-            out=of_a_node[:],
-            in_=ident[:].rearrange("r (a j) -> r a j", a=A_PER_TILE),
-            axis=AXIS_X,
-            op=ADD,
-        )
-        of_b_node = keep.tile([P, NB], F32)
-        nc.vector.tensor_reduce(
-            out=of_b_node[:],
-            in_=ident[:].rearrange("r (a j) -> r j a", a=A_PER_TILE),
-            axis=AXIS_X,
-            op=ADD,
-        )
-        summers = keep.tile([P, ROW_TILES, P], F32)
-        nc.vector.memset(summers[:], 0.0)
-        for rt in range(ROW_TILES):
-            first_a = rt * A_PER_TILE
-            nc.vector.tensor_copy(
-                out=summers[:, rt, first_a : first_a + A_PER_TILE], in_=of_a_node[:]
-            )
-        nc.vector.tensor_copy(
-            out=summers[:, :, NA : NA + NB],
-            in_=of_b_node[:].unsqueeze(1).to_broadcast([P, ROW_TILES, NB]),
+        node_cols = keep.tile([P, ED], BF16)
+        nc.scalar.copy(
+            out=node_cols[:].rearrange("p (g s m) -> p g s m", g=PASSES_2, s=PACK),
+            in_=node_rows[:].rearrange("p (g m s) -> p g s m", g=PASSES_2, s=PACK),
         )
 
         we_codes = keep.tile([P, PASSES_1 * ED], U32, align_bytes=64)
@@ -144,8 +134,8 @@ def tile_bipartiteneuralmessagepassinglayer_pa_kernel(
         we2_scales = keep.tile([P, PASSES_2 * ED], U8, align_bytes=64)
         x_codes = keep.tile([P, ROW_TILES * PASSES_1 * P], U32, align_bytes=64)
         x_scales = keep.tile([P, ROW_TILES * PASSES_1 * P], U8, align_bytes=64)
-        h_codes = keep.tile([P, ROW_TILES * PASSES_2 * P], U32, align_bytes=64)
-        h_scales = keep.tile([P, ROW_TILES * PASSES_2 * P], U8, align_bytes=64)
+        h_codes = keep.tile([P, PASSES_2 * ROWS], U32, align_bytes=64)
+        h_scales = keep.tile([P, PASSES_2 * ROWS], U8, align_bytes=64)
 
         pieces = []
         for half in range(OUT_HALVES):
@@ -157,26 +147,21 @@ def tile_bipartiteneuralmessagepassinglayer_pa_kernel(
                 pieces.append((we2_raw[:, g, :, cols], we2_codes, we2_scales, g * ED + half * BANK))
         grouped_of = {}
 
-        def regroup_piece(index):
+        def regroup_piece(index, vector_quarters):
             raw = pieces[index][0]
             grouped = grouped_w.tile([P, BANK * PACK], BF16, align_bytes=64)
             grouped_of[index] = grouped
             if index < OUT_HALVES * PASSES_1:
-                by_column = grouped[:].rearrange("p (s m t) -> p s m t", s=PACK, t=PACK)
-                by_raw = raw.rearrange("p t (m s) -> p s m t", s=PACK)
-                nc.vector.tensor_copy(out=by_column[:, 0:2], in_=by_raw[:, 0:2])
-                nc.scalar.copy(out=by_column[:, 2:4], in_=by_raw[:, 2:4])
-                return
-            by_column = grouped[:].rearrange("p (n t) -> p n t", t=PACK)
-            first, second = slice(0, BANK // 2), slice(BANK // 2, BANK)
-            nc.vector.tensor_copy(
-                out=by_column[:, first, :].rearrange("p (n i) t -> p n t i", i=4),
-                in_=raw[:, :, first].rearrange("p t (n i) -> p n t i", i=4),
-            )
-            nc.scalar.copy(
-                out=by_column[:, second, :].rearrange("p (n i) t -> p n t i", i=4),
-                in_=raw[:, :, second].rearrange("p t (n i) -> p n t i", i=4),
-            )
+                dst = grouped[:].rearrange("p (s m t) -> p s m t", s=PACK, t=PACK)
+                src = raw.rearrange("p t (m s) -> p s m t", s=PACK)
+            else:
+                dst = grouped[:].rearrange("p (n i t) -> p n t i", i=PACK, t=PACK)
+                src = raw.rearrange("p t (n i) -> p n t i", i=PACK)
+            cut = vector_quarters * dst.shape[1] // PACK
+            if cut > 0:
+                nc.vector.tensor_copy(out=dst[:, :cut], in_=src[:, :cut])
+            if cut < dst.shape[1]:
+                nc.scalar.copy(out=dst[:, cut:], in_=src[:, cut:])
 
         def quantise_piece(index):
             codes, scales, first_col = pieces[index][1:]
@@ -196,7 +181,7 @@ def tile_bipartiteneuralmessagepassinglayer_pa_kernel(
                 "p (c r u) -> p c r u", c=PASSES_1, u=2
             )
             for pair in range(PASSES_1 // 2):
-                xt = psum_x.tile([P, 4, P], F32)
+                xt = psum_tr.tile([P, 4, P], F32, tag="tr")
                 for quarter in range(4):
                     c, u = divmod(pair * 4 + quarter, 2)
                     first = rt * words_per_row + c * 2 * P
@@ -215,7 +200,7 @@ def tile_bipartiteneuralmessagepassinglayer_pa_kernel(
                 out=x_codes[:, cols].bitcast(FP8X4), scales=x_scales[:, cols], in_=grouped[:]
             )
 
-        def node_terms(rt, g):
+        def edge_terms(rt, g):
             terms_ps = psum_plain.tile([P, PACK, P], F32, tag="plain")
             for t in range(PACK):
                 e_tile = g * PACK + t
@@ -248,7 +233,10 @@ def tile_bipartiteneuralmessagepassinglayer_pa_kernel(
                     )
             h_grouped = hidden.tile([P, P, PACK], BF16, align_bytes=64)
             nc.vector.tensor_tensor(
-                out=h_grouped[:], in0=h_ps[:].rearrange("p t r -> p r t"), in1=terms[:], op=ADD
+                out=h_grouped[:],
+                in0=h_ps[:].rearrange("p t r -> p r t"),
+                in1=terms[:],
+                op=ADD,
             )
             return h_grouped
 
@@ -256,93 +244,193 @@ def tile_bipartiteneuralmessagepassinglayer_pa_kernel(
             nc.vector.tensor_scalar_max(out=h_grouped[:], in0=h_grouped[:], scalar1=0.0)
 
         def quantise_hidden(rt, g, h_grouped):
-            cols = slice((rt * PASSES_2 + g) * P, (rt * PASSES_2 + g + 1) * P)
+            cols = slice(g * ROWS + rt * P, g * ROWS + (rt + 1) * P)
             nc.vector.quantize_mx(
                 out=h_codes[:, cols].bitcast(FP8X4),
                 scales=h_scales[:, cols],
                 in_=h_grouped[:].rearrange("p r t -> p (r t)"),
             )
 
-        def second_product(rt):
-            latent = latent_pool.tile([P, ED], F32)
-            for half in range(OUT_HALVES):
-                o_ps = psum_mx.tile([P, BANK], F32, tag="mx")
+        be2_cols = keep.tile([P, OUT_TILES], F32)
+
+        def transpose_be2():
+            be2_ps = psum_plain.tile([P, OUT_TILES, 2], F32, tag="plain")
+            for ft in range(OUT_TILES):
+                nc.tensor.matmul(
+                    be2_ps[:, ft, :],
+                    lhsT=node_rows[:, ft * P : (ft + 1) * P],
+                    rhs=ident_bf[:, BE2_ROW : BE2_ROW + 2],
+                    start=True,
+                    stop=True,
+                )
+            nc.scalar.copy(out=be2_cols[:], in_=be2_ps[:, :, 0])
+
+        latent_of, natural_of = {}, {}
+        sum_b_parts = keep.tile([P, QUARTERS, OUT_TILES, NB], F32)
+
+        def second_product(rq, pair):
+            o_ps = psum_mx.tile([P, 2, Q_ROWS], F32, tag="mx")
+            for half in range(2):
+                ft = 2 * pair + half
                 for g in range(PASSES_2):
-                    r_cols = slice((rt * PASSES_2 + g) * P, (rt * PASSES_2 + g + 1) * P)
-                    f_cols = slice(g * ED + half * BANK, g * ED + (half + 1) * BANK)
+                    r_cols = slice(g * ROWS + rq * Q_ROWS, g * ROWS + (rq + 1) * Q_ROWS)
+                    f_cols = slice(g * ED + ft * P, g * ED + (ft + 1) * P)
                     nc.tensor.matmul_mx(
-                        out=o_ps[:],
-                        lhsT=h_codes[:, r_cols].bitcast(FP8X4),
-                        lhsT_scale=h_scales[:, r_cols],
-                        rhs=we2_codes[:, f_cols].bitcast(FP8X4),
-                        rhs_scale=we2_scales[:, f_cols],
+                        out=o_ps[:, half, :],
+                        lhsT=we2_codes[:, f_cols].bitcast(FP8X4),
+                        lhsT_scale=we2_scales[:, f_cols],
+                        rhs=h_codes[:, r_cols].bitcast(FP8X4),
+                        rhs_scale=h_scales[:, r_cols],
                         start=(g == 0),
                         stop=(g == PASSES_2 - 1),
                     )
-                cols = slice(half * BANK, (half + 1) * BANK)
-                nc.vector.tensor_tensor(
-                    out=latent[:, cols], in0=o_ps[:], in1=be2_all[:, cols], op=ADD
-                )
-                nc.scalar.activation(out=latent[:, cols], in_=latent[:, cols], func=RELU)
-            nc.sync.dma_start(out=latent_rows[rt * P : (rt + 1) * P, :], in_=latent[:])
-            return latent
-
-        def add_to_sums(rt, latent, sums_ps):
-            for half in range(OUT_HALVES):
-                nc.tensor.matmul(
-                    sums_ps[half][:],
-                    lhsT=summers[:, rt, :],
-                    rhs=latent[:, half * BANK : (half + 1) * BANK],
-                    start=(rt == 0),
-                    stop=(rt == ROW_TILES - 1),
+            latent = latent_pool.tile([P, 2, Q_ROWS], F32)
+            latent_of[rq, pair] = latent
+            for half in range(2):
+                ft = 2 * pair + half
+                nc.scalar.activation(
+                    out=latent[:, half, :],
+                    in_=o_ps[:, half, :],
+                    func=RELU,
+                    bias=be2_cols[:, ft : ft + 1],
                 )
 
-        for index in range(PASSES_1):
-            regroup_piece(index)
-            if index > 0:
-                quantise_piece(index - 1)
-        quantise_piece(PASSES_1 - 1)
+        def add_up_nodes(rq, pair):
+            latent = latent_of[rq, pair]
+            nc.vector.tensor_reduce(
+                out=sums_t[:, 2 * pair : 2 * pair + 2, rq * A_PER_QUARTER : (rq + 1) * A_PER_QUARTER],
+                in_=latent[:].rearrange("p f (i j) -> p f i j", j=NB),
+                axis=AXIS_X,
+                op=ADD,
+            )
+            engine = nc.gpsimd if rq < 3 else nc.vector
+            tree = trees.tile([P, 2, Q_ROWS], F32)
+            size = Q_ROWS // 2
+            before = latent[:]
+            while size >= NB:
+                if size == NB:
+                    after = sum_b_parts[:, rq, 2 * pair : 2 * pair + 2, :]
+                else:
+                    after = tree[:, :, Q_ROWS - 2 * size : Q_ROWS - size]
+                engine.tensor_tensor(
+                    out=after, in0=before[:, :, 0:size], in1=before[:, :, size : 2 * size], op=ADD
+                )
+                before = after
+                size //= 2
 
-        units = PASSES_2 * ROW_TILES
-        terms_of, h_of = {}, {}
-        for unit in range(-1, units + 1):
-            following, before = unit + 1, unit - 1
-            if following < units:
-                next_g, next_rt = divmod(following, ROW_TILES)
-                if next_g == 0:
-                    x_grouped = transpose_x(next_rt)
-                    quantise_x(next_rt, x_grouped)
-            if 0 <= unit < units:
-                g, rt = divmod(unit, ROW_TILES)
-                h_of[unit] = first_product(rt, g, terms_of[unit])
-            if following < units:
-                terms_of[following] = node_terms(next_rt, next_g)
+        def add_up_quarters(rq, pair):
+            fts = slice(2 * pair, 2 * pair + 2)
+            so_far = sum_b_parts[:, 0, fts, :] if rq == 1 else sums_t[:, fts, NA : NA + NB]
+            nc.vector.tensor_tensor(
+                out=sums_t[:, fts, NA : NA + NB], in0=so_far, in1=sum_b_parts[:, rq, fts, :], op=ADD
+            )
+
+        def transpose_out(rq, pair, copy):
+            if pair == 0:
+                natural = stores.tile([P, 2, ED], F32)
+                natural_of[rq] = natural
+            rows_ps = psum_tr.tile([P, 2, 2, P], F32, tag="tr")
+            for half in range(2):
+                for q in range(2):
+                    nc.tensor.transpose(
+                        rows_ps[:, q, half, :],
+                        latent_of[rq, pair][:, half, q * P : (q + 1) * P],
+                        ident[:],
+                    )
+            copy(
+                out=natural_of[rq][:, :, 2 * pair * P : 2 * (pair + 1) * P],
+                in_=rows_ps[:].rearrange("p q f r -> p q (f r)"),
+            )
+
+        def store(rq, first, last):
+            cols = slice(2 * first * P, 2 * last * P)
+            nc.sync.dma_start(
+                out=latent_rows[rq * Q_ROWS : (rq + 1) * Q_ROWS, cols].rearrange("(q p) f -> p q f", p=P),
+                in_=natural_of[rq][:, :, cols],
+            )
+
+        x_of, terms_of, h_of = {}, {}, {}
+        x_of[0] = transpose_x(0)
+        quantise_x(0, x_of[0])
+        transpose_be2()
+        regroup_piece(0, 2)
+        terms_of[0, 0] = edge_terms(0, 0)
+        regroup_piece(1, 2)
+        quantise_piece(0)
+        terms_of[0, 1] = edge_terms(1, 0)
+        regroup_piece(2, 2)
+        quantise_piece(1)
+        x_of[1] = transpose_x(1)
+        regroup_piece(3, 2)
+        quantise_piece(2)
+        quantise_x(1, x_of[1])
+        quantise_piece(3)
+
+        n1 = 5
+        units = [(0, rt) for rt in range(n1)] + [(1, 0), (1, 1)]
+        done = [n1, 2]
+        while done[1] < 8:
+            for g in (1, 1, 0, 0):
+                if done[g] < 8:
+                    units.append((g, done[g]))
+                    done[g] += 1
+        AHEAD = 2
+        out_units = []
+
+        def finish(item):
+            rq, pair = item
+            transpose_out(rq, pair, nc.scalar.copy if (rq * 4 + pair) % 1 < 1 else nc.vector.tensor_copy)
+            add_up_nodes(rq, pair)
+            if rq > 0:
+                add_up_quarters(rq, pair)
+            if pair % 2 == 1:
+                store(rq, pair - 1, pair + 1)
+
+        counts = {"made": 0, "finished": 0}
+
+        def out_step():
+            if counts["made"] < len(out_units):
+                second_product(*out_units[counts["made"]])
+                counts["made"] += 1
+            behind = 1 if counts["made"] < len(out_units) else 0
+            if counts["made"] - counts["finished"] > behind:
+                finish(out_units[counts["finished"]])
+                counts["finished"] += 1
+
+        for unit in range(len(units) + 1):
+            following, before = unit + AHEAD, unit - 1
+            if unit < len(units):
+                g, rt = units[unit]
+                if following < len(units):
+                    next_g, next_rt = units[following]
+                    if next_g == 0:
+                        x_of[next_rt] = transpose_x(next_rt)
+                    terms_of[next_g, next_rt] = edge_terms(next_rt, next_g)
+                if 1 <= unit <= 8:
+                    quantise_piece(PASSES_1 + unit - 1)
+                h_of[unit] = first_product(rt, g, terms_of[g, rt])
+                if unit < 8:
+                    regroup_piece(PASSES_1 + unit, 2 if unit < 4 else 2)
+                if following < len(units) and next_g == 0:
+                    quantise_x(next_rt, x_of[next_rt])
             if before >= 0:
                 relu_hidden(h_of[before])
-            if 0 <= unit < units:
-                index = PASSES_1 + unit // 2
-                if unit % 2 == 0:
-                    regroup_piece(index)
-                else:
-                    quantise_piece(index)
-            if before >= 0:
-                g, rt = divmod(before, ROW_TILES)
+                g, rt = units[before]
                 quantise_hidden(rt, g, h_of[before])
-
-        SUMS_BEHIND = 2
-        sums_ps = []
-        for half in range(OUT_HALVES):
-            half_ps = psum_plain.tile([P, BANK], F32, tag="plain")
-            sums_ps.append(half_ps)
-        latent_of = {}
-        for rt in range(ROW_TILES + SUMS_BEHIND):
-            if rt < ROW_TILES:
-                latent_of[rt] = second_product(rt)
-            if rt >= SUMS_BEHIND:
-                add_to_sums(rt - SUMS_BEHIND, latent_of[rt - SUMS_BEHIND], sums_ps)
+                if g == 1 and rt % 2 == 1:
+                    out_units.extend([(rt // 2, pair) for pair in range(4)])
+            if unit >= 9:
+                for rep in range(2):
+                    out_step()
+        while counts["finished"] < len(out_units):
+            out_step()
 
         sums = keep.tile([P, ED], F32)
-        nc.vector.tensor_copy(out=sums[:, 0:BANK], in_=sums_ps[0][:])
-        nc.scalar.copy(out=sums[:, BANK:ED], in_=sums_ps[1][:])
+        for half in range(OUT_HALVES):
+            sums_ps = psum_tr.tile([P, 4, P], F32, tag="tr")
+            for q in range(4):
+                nc.tensor.transpose(sums_ps[:, q, :], sums_t[:, half * 4 + q, :], ident[:])
+            copy = nc.vector.tensor_copy if half == 0 else nc.scalar.copy
+            copy(out=sums[:, half * BANK : (half + 1) * BANK], in_=sums_ps[:].rearrange("p q f -> p (q f)"))
         nc.sync.dma_start(out=out_1, in_=sums[0:NA, :])
         nc.sync.dma_start(out=out_2, in_=sums[NA : NA + NB, :])

@@ -45,8 +45,9 @@ def tile_bipartiteneuralmessagepassinglayer_pa_kernel(
     with ExitStack() as ctx:
         keep = ctx.enter_context(tc.tile_pool(name="keep", bufs=1))
         grouped_w = ctx.enter_context(tc.tile_pool(name="grouped_w", bufs=3))
-        grouped_x = ctx.enter_context(tc.tile_pool(name="grouped_x", bufs=3))
-        terms_pool = ctx.enter_context(tc.tile_pool(name="terms", bufs=6))
+        grouped_x = ctx.enter_context(tc.tile_pool(name="grouped_x", bufs=4))
+        terms_pool = ctx.enter_context(tc.tile_pool(name="terms", bufs=4))
+        sums_h = ctx.enter_context(tc.tile_pool(name="sums_h", bufs=2))
         hidden = ctx.enter_context(tc.tile_pool(name="hidden", bufs=3))
         latent_pool = ctx.enter_context(tc.tile_pool(name="latent", bufs=4))
         trees = ctx.enter_context(tc.tile_pool(name="trees", bufs=2))
@@ -78,11 +79,11 @@ def tile_bipartiteneuralmessagepassinglayer_pa_kernel(
         nc.sync.dma_start(out=node_rows[NA : NA + NB, :], in_=b_proj)
         nc.sync.dma_start(out=node_rows[BE1_ROW:BE2_ROW, :], in_=be1.partition_broadcast(BE2_ROW - BE1_ROW))
         nc.sync.dma_start(out=node_rows[BE2_ROW:P, :], in_=be2.partition_broadcast(P - BE2_ROW))
-        load_we_piece(0, 1)
         load_x(0)
+        load_we_piece(0, 1)
+        load_x(1)
         load_we_piece(0, 2)
         load_we_piece(0, 3)
-        load_x(1)
         load_x(2)
         load_x(3)
         load_we_piece(1, 0)
@@ -90,6 +91,7 @@ def tile_bipartiteneuralmessagepassinglayer_pa_kernel(
         load_we_piece(1, 2)
         load_we_piece(1, 3)
         load_x(4)
+        load_x(5)
         nc.sync.dma_start(
             out=we2_raw[:, 0],
             in_=We2[0 * K_PASS : 1 * K_PASS, :].rearrange("(p t) n -> p t n", t=PACK),
@@ -98,7 +100,6 @@ def tile_bipartiteneuralmessagepassinglayer_pa_kernel(
             out=we2_raw[:, 1],
             in_=We2[1 * K_PASS : 2 * K_PASS, :].rearrange("(p t) n -> p t n", t=PACK),
         )
-        load_x(5)
         load_x(6)
         load_x(7)
 
@@ -132,8 +133,8 @@ def tile_bipartiteneuralmessagepassinglayer_pa_kernel(
         we_scales = keep.tile([P, PASSES_1 * ED], U8, align_bytes=64)
         we2_codes = keep.tile([P, PASSES_2 * ED], U32, align_bytes=64)
         we2_scales = keep.tile([P, PASSES_2 * ED], U8, align_bytes=64)
-        x_codes = keep.tile([P, ROW_TILES * PASSES_1 * P], U32, align_bytes=64)
-        x_scales = keep.tile([P, ROW_TILES * PASSES_1 * P], U8, align_bytes=64)
+        x_codes = keep.tile([P, PASSES_1 * ROWS], U32, align_bytes=64)
+        x_scales = keep.tile([P, PASSES_1 * ROWS], U8, align_bytes=64)
         h_codes = keep.tile([P, PASSES_2 * ROWS], U32, align_bytes=64)
         h_scales = keep.tile([P, PASSES_2 * ROWS], U8, align_bytes=64)
 
@@ -175,53 +176,56 @@ def tile_bipartiteneuralmessagepassinglayer_pa_kernel(
         x_words = x_raw[:].bitcast(F32)
         words_per_row = K1 // 2
 
-        def transpose_x(rt):
-            grouped = grouped_x.tile([P, PASSES_1 * P * PACK], BF16, align_bytes=64)
+        def transpose_x(rq, pair):
+            grouped = grouped_x.tile([P, 2 * Q_ROWS * PACK], BF16, align_bytes=64)
             grouped_words = grouped[:].bitcast(F32).rearrange(
-                "p (c r u) -> p c r u", c=PASSES_1, u=2
+                "p (c q r u) -> p q c r u", c=2, q=2, u=2
             )
-            for pair in range(PASSES_1 // 2):
+            for q in range(2):
+                first_word = (2 * rq + q) * words_per_row
                 xt = psum_tr.tile([P, 4, P], F32, tag="tr")
                 for quarter in range(4):
                     c, u = divmod(pair * 4 + quarter, 2)
-                    first = rt * words_per_row + c * 2 * P
+                    first = first_word + c * 2 * P
                     nc.tensor.transpose(
                         xt[:, quarter, :], x_words[:, first + u : first + 2 * P : 2], ident[:]
                     )
                 nc.scalar.copy(
-                    out=grouped_words[:, 2 * pair : 2 * pair + 2, :, :],
+                    out=grouped_words[:, q],
                     in_=xt[:].rearrange("p (c u) r -> p c r u", u=2),
                 )
             return grouped
 
-        def quantise_x(rt, grouped):
-            cols = slice(rt * PASSES_1 * P, (rt + 1) * PASSES_1 * P)
+        def quantise_x(rq, pair, grouped):
+            first = (rq * PASSES_1 + 2 * pair) * Q_ROWS
+            cols = slice(first, first + 2 * Q_ROWS)
             nc.vector.quantize_mx(
                 out=x_codes[:, cols].bitcast(FP8X4), scales=x_scales[:, cols], in_=grouped[:]
             )
 
-        def edge_terms(rt, g):
-            terms_ps = psum_plain.tile([P, PACK, P], F32, tag="plain")
-            for t in range(PACK):
-                e_tile = g * PACK + t
+        def edge_terms(rq, g, tp):
+            terms_ps = psum_plain.tile([P, 2, Q_ROWS], F32, tag="plain")
+            for t in range(2):
+                e_tile = g * PACK + 2 * tp + t
                 nc.tensor.matmul(
                     terms_ps[:, t, :],
                     lhsT=node_cols[:, e_tile * P : (e_tile + 1) * P],
-                    rhs=pick_cols[:, rt * P : (rt + 1) * P],
+                    rhs=pick_cols[:, rq * Q_ROWS : (rq + 1) * Q_ROWS],
                     start=True,
                     stop=True,
                 )
-            terms = terms_pool.tile([P, P, PACK], F32)
-            nc.scalar.copy(out=terms[:], in_=terms_ps[:].rearrange("p t r -> p r t"))
+            terms = terms_pool.tile([P, 2, Q_ROWS], F32)
+            nc.scalar.copy(out=terms[:], in_=terms_ps[:])
             return terms
 
-        def first_product(rt, g, terms):
-            h_ps = psum_mx.tile([P, PACK, P], F32, tag="mx")
-            for t in range(PACK):
-                e_tile = g * PACK + t
+        def first_product(rq, g, tp, terms, before_relu):
+            h_ps = psum_mx.tile([P, 2, Q_ROWS], F32, tag="mx")
+            for t in range(2):
+                e_tile = g * PACK + 2 * tp + t
                 for c in range(PASSES_1):
                     w_cols = slice(c * ED + e_tile * P, c * ED + (e_tile + 1) * P)
-                    r_cols = slice((rt * PASSES_1 + c) * P, (rt * PASSES_1 + c + 1) * P)
+                    first = (rq * PASSES_1 + c) * Q_ROWS
+                    r_cols = slice(first, first + Q_ROWS)
                     nc.tensor.matmul_mx(
                         out=h_ps[:, t, :],
                         lhsT=we_codes[:, w_cols].bitcast(FP8X4),
@@ -231,24 +235,23 @@ def tile_bipartiteneuralmessagepassinglayer_pa_kernel(
                         start=(c == 0),
                         stop=(c == PASSES_1 - 1),
                     )
-            h_grouped = hidden.tile([P, P, PACK], BF16, align_bytes=64)
             nc.vector.tensor_tensor(
-                out=h_grouped[:],
-                in0=h_ps[:].rearrange("p t r -> p r t"),
-                in1=terms[:],
-                op=ADD,
+                out=before_relu[:, 2 * tp : 2 * tp + 2, :], in0=h_ps[:], in1=terms[:], op=ADD
             )
-            return h_grouped
 
-        def relu_hidden(h_grouped):
-            nc.vector.tensor_scalar_max(out=h_grouped[:], in0=h_grouped[:], scalar1=0.0)
+        def relu_hidden(before_relu):
+            grouped = hidden.tile([P, Q_ROWS, PACK], BF16, align_bytes=64)
+            nc.vector.tensor_scalar_max(
+                out=grouped[:], in0=before_relu[:].rearrange("p t r -> p r t"), scalar1=0.0
+            )
+            return grouped
 
-        def quantise_hidden(rt, g, h_grouped):
-            cols = slice(g * ROWS + rt * P, g * ROWS + (rt + 1) * P)
+        def quantise_hidden(rq, g, grouped):
+            cols = slice(g * ROWS + rq * Q_ROWS, g * ROWS + (rq + 1) * Q_ROWS)
             nc.vector.quantize_mx(
                 out=h_codes[:, cols].bitcast(FP8X4),
                 scales=h_scales[:, cols],
-                in_=h_grouped[:].rearrange("p r t -> p (r t)"),
+                in_=grouped[:].rearrange("p r t -> p (r t)"),
             )
 
         be2_cols = keep.tile([P, OUT_TILES], F32)
@@ -349,32 +352,34 @@ def tile_bipartiteneuralmessagepassinglayer_pa_kernel(
                 in_=natural_of[rq][:, :, cols],
             )
 
-        x_of, terms_of, h_of = {}, {}, {}
-        x_of[0] = transpose_x(0)
-        quantise_x(0, x_of[0])
+        x_of, terms_of, hidden_of = {}, {}, {}
+
+        def transpose_quarter(rq):
+            for pair in range(PASSES_1 // 2):
+                x_of[rq, pair] = transpose_x(rq, pair)
+
+        def quantise_quarter(rq):
+            for pair in range(PASSES_1 // 2):
+                quantise_x(rq, pair, x_of[rq, pair])
+
+        units = [(0, 0), (0, 1), (1, 0), (0, 2), (1, 1), (0, 3), (1, 2), (1, 3)]
+        pieces_before = {1: [4, 5], 2: [6, 7], 3: [8, 9], 4: [10, 11]}
+        pieces_in = {0: [4, 5], 1: [6, 7], 2: [8, 9], 3: [10, 11]}
+        AHEAD = 1
+        transpose_quarter(0)
         transpose_be2()
         regroup_piece(0, 2)
-        terms_of[0, 0] = edge_terms(0, 0)
+        for tp in range(2):
+            terms_of[0, tp] = edge_terms(0, 0, tp)
         regroup_piece(1, 2)
         quantise_piece(0)
-        terms_of[0, 1] = edge_terms(1, 0)
         regroup_piece(2, 2)
         quantise_piece(1)
-        x_of[1] = transpose_x(1)
+        quantise_quarter(0)
         regroup_piece(3, 2)
         quantise_piece(2)
-        quantise_x(1, x_of[1])
         quantise_piece(3)
 
-        n1 = 5
-        units = [(0, rt) for rt in range(n1)] + [(1, 0), (1, 1)]
-        done = [n1, 2]
-        while done[1] < 8:
-            for g in (1, 1, 0, 0):
-                if done[g] < 8:
-                    units.append((g, done[g]))
-                    done[g] += 1
-        AHEAD = 2
         out_units = []
 
         def finish(item):
@@ -400,27 +405,30 @@ def tile_bipartiteneuralmessagepassinglayer_pa_kernel(
         for unit in range(len(units) + 1):
             following, before = unit + AHEAD, unit - 1
             if unit < len(units):
-                g, rt = units[unit]
+                g, rq = units[unit]
+                for index in pieces_before.get(unit, []):
+                    quantise_piece(index)
                 if following < len(units):
-                    next_g, next_rt = units[following]
+                    next_g, next_rq = units[following]
                     if next_g == 0:
-                        x_of[next_rt] = transpose_x(next_rt)
-                    terms_of[next_g, next_rt] = edge_terms(next_rt, next_g)
-                if 1 <= unit <= 8:
-                    quantise_piece(PASSES_1 + unit - 1)
-                h_of[unit] = first_product(rt, g, terms_of[g, rt])
-                if unit < 8:
-                    regroup_piece(PASSES_1 + unit, 2 if unit < 4 else 2)
+                        transpose_quarter(next_rq)
+                before_relu = sums_h.tile([P, PACK, Q_ROWS], BF16)
+                hidden_of[unit] = before_relu
+                for tp in range(2):
+                    first_product(rq, g, tp, terms_of[unit, tp], before_relu)
+                    if following < len(units):
+                        terms_of[following, tp] = edge_terms(next_rq, next_g, tp)
+                for index in pieces_in.get(unit, []):
+                    regroup_piece(index, 2 if index < 8 else 2)
                 if following < len(units) and next_g == 0:
-                    quantise_x(next_rt, x_of[next_rt])
+                    quantise_quarter(next_rq)
             if before >= 0:
-                relu_hidden(h_of[before])
-                g, rt = units[before]
-                quantise_hidden(rt, g, h_of[before])
-                if g == 1 and rt % 2 == 1:
-                    out_units.extend([(rt // 2, pair) for pair in range(4)])
-            if unit >= 9:
-                for rep in range(2):
+                g, rq = units[before]
+                quantise_hidden(rq, g, relu_hidden(hidden_of[before]))
+                if g == 1:
+                    out_units.extend([(rq, pair) for pair in range(4)])
+            for step in range(2):
+                if unit >= 4:
                     out_step()
         while counts["finished"] < len(out_units):
             out_step()

@@ -49,12 +49,14 @@ def tile_bipartiteneuralmessagepassinglayer_pa_kernel(
         terms_pool = ctx.enter_context(tc.tile_pool(name="terms", bufs=4))
         sums_h = ctx.enter_context(tc.tile_pool(name="sums_h", bufs=2))
         hidden = ctx.enter_context(tc.tile_pool(name="hidden", bufs=3))
-        latent_pool = ctx.enter_context(tc.tile_pool(name="latent", bufs=4))
-        trees = ctx.enter_context(tc.tile_pool(name="trees", bufs=2))
+        latent_pool = ctx.enter_context(tc.tile_pool(name="latent", bufs=5))
+        trees = ctx.enter_context(tc.tile_pool(name="trees", bufs=3))
         stores = ctx.enter_context(tc.tile_pool(name="stores", bufs=2))
         psum_tr = ctx.enter_context(tc.psum_pool(name="psum_tr", bufs=2))
         psum_plain = ctx.enter_context(tc.psum_pool(name="psum_plain", bufs=2))
         psum_mx = ctx.enter_context(tc.psum_pool(name="psum_mx", bufs=4))
+
+        ctx.enter_context(tc.manual_schedule())
 
         node_rows = keep.tile([P, ED], BF16)
         we_raw = keep.tile([P, OUT_HALVES, PASSES_1, PACK, BANK], BF16)
@@ -75,11 +77,11 @@ def tile_bipartiteneuralmessagepassinglayer_pa_kernel(
             )
 
         load_we_piece(0, 0)
+        load_x(0)
         nc.sync.dma_start(out=node_rows[0:NA, :], in_=a_proj)
         nc.sync.dma_start(out=node_rows[NA : NA + NB, :], in_=b_proj)
         nc.sync.dma_start(out=node_rows[BE1_ROW:BE2_ROW, :], in_=be1.partition_broadcast(BE2_ROW - BE1_ROW))
         nc.sync.dma_start(out=node_rows[BE2_ROW:P, :], in_=be2.partition_broadcast(P - BE2_ROW))
-        load_x(0)
         load_we_piece(0, 1)
         load_x(1)
         load_we_piece(0, 2)
@@ -91,11 +93,11 @@ def tile_bipartiteneuralmessagepassinglayer_pa_kernel(
         load_we_piece(1, 2)
         load_we_piece(1, 3)
         load_x(4)
-        load_x(5)
         nc.sync.dma_start(
             out=we2_raw[:, 0],
             in_=We2[0 * K_PASS : 1 * K_PASS, :].rearrange("(p t) n -> p t n", t=PACK),
         )
+        load_x(5)
         nc.sync.dma_start(
             out=we2_raw[:, 1],
             in_=We2[1 * K_PASS : 2 * K_PASS, :].rearrange("(p t) n -> p t n", t=PACK),
@@ -123,12 +125,6 @@ def tile_bipartiteneuralmessagepassinglayer_pa_kernel(
             out=pick[:], in0=pick[:], scalar1=ident[:, NA + NB : NA + NB + 1]
         )
         pick_cols = pick[:].rearrange("k i j -> k (i j)")
-        node_cols = keep.tile([P, ED], BF16)
-        nc.scalar.copy(
-            out=node_cols[:].rearrange("p (g s m) -> p g s m", g=PASSES_2, s=PACK),
-            in_=node_rows[:].rearrange("p (g m s) -> p g s m", g=PASSES_2, s=PACK),
-        )
-
         we_codes = keep.tile([P, PASSES_1 * ED], U32, align_bytes=64)
         we_scales = keep.tile([P, PASSES_1 * ED], U8, align_bytes=64)
         we2_codes = keep.tile([P, PASSES_2 * ED], U32, align_bytes=64)
@@ -148,21 +144,27 @@ def tile_bipartiteneuralmessagepassinglayer_pa_kernel(
                 pieces.append((we2_raw[:, g, :, cols], we2_codes, we2_scales, g * ED + half * BANK))
         grouped_of = {}
 
-        def regroup_piece(index, vector_quarters):
+        def regroup_piece(index, vector_eighths):
             raw = pieces[index][0]
             grouped = grouped_w.tile([P, BANK * PACK], BF16, align_bytes=64)
             grouped_of[index] = grouped
+            cut = vector_eighths * P // 8
             if index < OUT_HALVES * PASSES_1:
                 dst = grouped[:].rearrange("p (s m t) -> p s m t", s=PACK, t=PACK)
                 src = raw.rearrange("p t (m s) -> p s m t", s=PACK)
+                vector_part, scalar_part = (
+                    (slice(None), slice(None), part) for part in (slice(0, cut), slice(cut, P))
+                )
             else:
                 dst = grouped[:].rearrange("p (n i t) -> p n t i", i=PACK, t=PACK)
                 src = raw.rearrange("p t (n i) -> p n t i", i=PACK)
-            cut = vector_quarters * dst.shape[1] // PACK
+                vector_part, scalar_part = (
+                    (slice(None), part) for part in (slice(0, cut), slice(cut, P))
+                )
             if cut > 0:
-                nc.vector.tensor_copy(out=dst[:, :cut], in_=src[:, :cut])
-            if cut < dst.shape[1]:
-                nc.scalar.copy(out=dst[:, cut:], in_=src[:, cut:])
+                nc.vector.tensor_copy(out=dst[vector_part], in_=src[vector_part])
+            if cut < P:
+                nc.scalar.copy(out=dst[scalar_part], in_=src[scalar_part])
 
         def quantise_piece(index):
             codes, scales, first_col = pieces[index][1:]
@@ -176,40 +178,39 @@ def tile_bipartiteneuralmessagepassinglayer_pa_kernel(
         x_words = x_raw[:].bitcast(F32)
         words_per_row = K1 // 2
 
-        def transpose_x(rq, pair):
-            grouped = grouped_x.tile([P, 2 * Q_ROWS * PACK], BF16, align_bytes=64)
-            grouped_words = grouped[:].bitcast(F32).rearrange(
+        grouped_of_x = {}
+
+        def transpose_x(rq, pair, q, copy):
+            if (rq, pair) not in grouped_of_x:
+                grouped = grouped_x.tile([P, 2 * Q_ROWS * PACK], BF16, align_bytes=64)
+                grouped_of_x[rq, pair] = grouped
+            grouped_words = grouped_of_x[rq, pair][:].bitcast(F32).rearrange(
                 "p (c q r u) -> p q c r u", c=2, q=2, u=2
             )
-            for q in range(2):
-                first_word = (2 * rq + q) * words_per_row
-                xt = psum_tr.tile([P, 4, P], F32, tag="tr")
-                for quarter in range(4):
-                    c, u = divmod(pair * 4 + quarter, 2)
-                    first = first_word + c * 2 * P
-                    nc.tensor.transpose(
-                        xt[:, quarter, :], x_words[:, first + u : first + 2 * P : 2], ident[:]
-                    )
-                nc.scalar.copy(
-                    out=grouped_words[:, q],
-                    in_=xt[:].rearrange("p (c u) r -> p c r u", u=2),
+            first_word = (2 * rq + q) * words_per_row
+            xt = psum_tr.tile([P, 4, P], F32, tag="tr")
+            for quarter in range(4):
+                c, u = divmod(pair * 4 + quarter, 2)
+                first = first_word + c * 2 * P
+                nc.tensor.transpose(
+                    xt[:, quarter, :], x_words[:, first + u : first + 2 * P : 2], ident[:]
                 )
-            return grouped
+            copy(out=grouped_words[:, q], in_=xt[:].rearrange("p (c u) r -> p c r u", u=2))
 
-        def quantise_x(rq, pair, grouped):
+        def quantise_x(rq, pair):
             first = (rq * PASSES_1 + 2 * pair) * Q_ROWS
             cols = slice(first, first + 2 * Q_ROWS)
             nc.vector.quantize_mx(
-                out=x_codes[:, cols].bitcast(FP8X4), scales=x_scales[:, cols], in_=grouped[:]
+                out=x_codes[:, cols].bitcast(FP8X4), scales=x_scales[:, cols], in_=grouped_of_x[rq, pair][:]
             )
 
         def edge_terms(rq, g, tp):
             terms_ps = psum_plain.tile([P, 2, Q_ROWS], F32, tag="plain")
             for t in range(2):
-                e_tile = g * PACK + 2 * tp + t
+                first = g * K_PASS + 2 * tp + t
                 nc.tensor.matmul(
                     terms_ps[:, t, :],
-                    lhsT=node_cols[:, e_tile * P : (e_tile + 1) * P],
+                    lhsT=node_rows[:, first : (g + 1) * K_PASS : PACK],
                     rhs=pick_cols[:, rq * Q_ROWS : (rq + 1) * Q_ROWS],
                     start=True,
                     stop=True,
@@ -218,7 +219,7 @@ def tile_bipartiteneuralmessagepassinglayer_pa_kernel(
             nc.scalar.copy(out=terms[:], in_=terms_ps[:])
             return terms
 
-        def first_product(rq, g, tp, terms, before_relu):
+        def first_product(rq, g, tp):
             h_ps = psum_mx.tile([P, 2, Q_ROWS], F32, tag="mx")
             for t in range(2):
                 e_tile = g * PACK + 2 * tp + t
@@ -235,6 +236,9 @@ def tile_bipartiteneuralmessagepassinglayer_pa_kernel(
                         start=(c == 0),
                         stop=(c == PASSES_1 - 1),
                     )
+            return h_ps
+
+        def add_terms(h_ps, tp, terms, before_relu):
             nc.vector.tensor_tensor(
                 out=before_relu[:, 2 * tp : 2 * tp + 2, :], in0=h_ps[:], in1=terms[:], op=ADD
             )
@@ -269,7 +273,6 @@ def tile_bipartiteneuralmessagepassinglayer_pa_kernel(
             nc.scalar.copy(out=be2_cols[:], in_=be2_ps[:, :, 0])
 
         latent_of, natural_of = {}, {}
-        sum_b_parts = keep.tile([P, QUARTERS, OUT_TILES, NB], F32)
 
         def second_product(rq, pair):
             o_ps = psum_mx.tile([P, 2, Q_ROWS], F32, tag="mx")
@@ -298,6 +301,9 @@ def tile_bipartiteneuralmessagepassinglayer_pa_kernel(
                     bias=be2_cols[:, ft : ft + 1],
                 )
 
+        def on_gpsimd(rq, pair):
+            return pair % 2 == 0
+
         def add_up_nodes(rq, pair):
             latent = latent_of[rq, pair]
             nc.vector.tensor_reduce(
@@ -306,26 +312,55 @@ def tile_bipartiteneuralmessagepassinglayer_pa_kernel(
                 axis=AXIS_X,
                 op=ADD,
             )
-            engine = nc.gpsimd if rq < 3 else nc.vector
+
+        halved_of = {}
+
+        def halve_nodes(rq, pair):
+            latent = latent_of[rq, pair]
             tree = trees.tile([P, 2, Q_ROWS], F32)
+            halved_of[rq, pair] = tree
+            fts = slice(2 * pair, 2 * pair + 2)
+            if not on_gpsimd(rq, pair):
+                nc.vector.tensor_tensor(
+                    out=tree[:, :, 0 : Q_ROWS // 2],
+                    in0=latent[:, :, 0 : Q_ROWS // 2],
+                    in1=latent[:, :, Q_ROWS // 2 : Q_ROWS],
+                    op=ADD,
+                )
+                return
             size = Q_ROWS // 2
             before = latent[:]
             while size >= NB:
-                if size == NB:
-                    after = sum_b_parts[:, rq, 2 * pair : 2 * pair + 2, :]
+                if size == NB and rq == 0:
+                    after = sums_t[:, fts, NA : NA + NB]
                 else:
                     after = tree[:, :, Q_ROWS - 2 * size : Q_ROWS - size]
-                engine.tensor_tensor(
+                nc.gpsimd.tensor_tensor(
                     out=after, in0=before[:, :, 0:size], in1=before[:, :, size : 2 * size], op=ADD
                 )
                 before = after
                 size //= 2
+            if rq > 0:
+                so_far = sums_t[:, fts, NA : NA + NB]
+                nc.gpsimd.tensor_tensor(out=so_far, in0=so_far, in1=before, op=ADD)
 
-        def add_up_quarters(rq, pair):
-            fts = slice(2 * pair, 2 * pair + 2)
-            so_far = sum_b_parts[:, 0, fts, :] if rq == 1 else sums_t[:, fts, NA : NA + NB]
+        def add_the_halves(rq, pair):
+            if on_gpsimd(rq, pair):
+                return
+            tree = halved_of[rq, pair]
+            nc.vector.tensor_reduce(
+                out=tree[:, :, Q_ROWS - NB : Q_ROWS],
+                in_=tree[:, :, 0 : Q_ROWS // 2].rearrange("p f (i j) -> p f j i", j=NB),
+                axis=AXIS_X,
+                op=ADD,
+            )
+
+        def add_to_quarters(rq, pair):
+            if on_gpsimd(rq, pair):
+                return
+            so_far = sums_t[:, 2 * pair : 2 * pair + 2, NA : NA + NB]
             nc.vector.tensor_tensor(
-                out=sums_t[:, fts, NA : NA + NB], in0=so_far, in1=sum_b_parts[:, rq, fts, :], op=ADD
+                out=so_far, in0=so_far, in1=halved_of[rq, pair][:, :, Q_ROWS - NB : Q_ROWS], op=ADD
             )
 
         def transpose_out(rq, pair, copy):
@@ -352,93 +387,117 @@ def tile_bipartiteneuralmessagepassinglayer_pa_kernel(
                 in_=natural_of[rq][:, :, cols],
             )
 
-        x_of, terms_of, hidden_of = {}, {}, {}
+        vcopy, scopy = nc.vector.tensor_copy, nc.scalar.copy
+        terms_of, h_of, before_of, hidden_of = {}, {}, {}, {}
+        units = [(0, 0), (0, 1), (1, 0), (1, 1), (0, 2), (1, 2), (0, 3), (1, 3)]
+        beats = [(g, rq, tp) for g, rq in units for tp in range(2)]
+        x_banks = {}
+        for rq, first, per in [(1, 0, 2), (2, 5, 2), (3, 8, 1)]:
+            for index in range(4):
+                x_banks.setdefault(first + index // per, []).append((rq, index // 2, index % 2))
+        pieces_at = {0: [4], 1: [5, 6], 2: [7], 3: [8], 4: [9], 5: [10], 6: [11]}
+        out_at = {8: 1, 9: 1, 10: 1, 11: 2, 12: 1, 13: 1, 14: 2, 15: 1}
+        out_list = [(rq, pair) for rq in range(QUARTERS) for pair in range(4)]
 
-        def transpose_quarter(rq):
-            for pair in range(PASSES_1 // 2):
-                x_of[rq, pair] = transpose_x(rq, pair)
-
-        def quantise_quarter(rq):
-            for pair in range(PASSES_1 // 2):
-                quantise_x(rq, pair, x_of[rq, pair])
-
-        units = [(0, 0), (0, 1), (1, 0), (0, 2), (1, 1), (0, 3), (1, 2), (1, 3)]
-        pieces_before = {1: [4, 5], 2: [6, 7], 3: [8, 9], 4: [10, 11]}
-        pieces_in = {0: [4, 5], 1: [6, 7], 2: [8, 9], 3: [10, 11]}
-        AHEAD = 1
-        transpose_quarter(0)
-        transpose_be2()
-        regroup_piece(0, 2)
-        for tp in range(2):
-            terms_of[0, tp] = edge_terms(0, 0, tp)
-        regroup_piece(1, 2)
+        transpose_x(0, 0, 0, scopy)
+        regroup_piece(0, 6)
+        transpose_x(0, 1, 0, scopy)
+        terms_of[0] = edge_terms(0, 0, 0)
+        regroup_piece(1, 6)
         quantise_piece(0)
-        regroup_piece(2, 2)
+        transpose_x(0, 0, 1, scopy)
+        regroup_piece(2, 6)
         quantise_piece(1)
-        quantise_quarter(0)
-        regroup_piece(3, 2)
+        transpose_x(0, 1, 1, scopy)
+        quantise_x(0, 0)
+        regroup_piece(3, 6)
         quantise_piece(2)
+        quantise_x(0, 1)
         quantise_piece(3)
-
-        out_units = []
-
-        def finish(item):
-            rq, pair = item
-            transpose_out(rq, pair, nc.scalar.copy if (rq * 4 + pair) % 1 < 1 else nc.vector.tensor_copy)
-            add_up_nodes(rq, pair)
-            if rq > 0:
-                add_up_quarters(rq, pair)
-            if pair % 2 == 1:
-                store(rq, pair - 1, pair + 1)
-
-        counts = {"made": 0, "finished": 0}
-
-        def out_step():
-            if counts["made"] < len(out_units):
-                second_product(*out_units[counts["made"]])
-                counts["made"] += 1
-            behind = 1 if counts["made"] < len(out_units) else 0
-            if counts["made"] - counts["finished"] > behind:
-                finish(out_units[counts["finished"]])
-                counts["finished"] += 1
-
-        for unit in range(len(units) + 1):
-            following, before = unit + AHEAD, unit - 1
-            if unit < len(units):
-                g, rq = units[unit]
-                for index in pieces_before.get(unit, []):
-                    quantise_piece(index)
-                if following < len(units):
-                    next_g, next_rq = units[following]
-                    if next_g == 0:
-                        transpose_quarter(next_rq)
-                before_relu = sums_h.tile([P, PACK, Q_ROWS], BF16)
-                hidden_of[unit] = before_relu
-                for tp in range(2):
-                    first_product(rq, g, tp, terms_of[unit, tp], before_relu)
-                    if following < len(units):
-                        terms_of[following, tp] = edge_terms(next_rq, next_g, tp)
-                for index in pieces_in.get(unit, []):
-                    regroup_piece(index, 2 if index < 8 else 2)
-                if following < len(units) and next_g == 0:
-                    quantise_quarter(next_rq)
-            if before >= 0:
-                g, rq = units[before]
-                quantise_hidden(rq, g, relu_hidden(hidden_of[before]))
-                if g == 1:
-                    out_units.extend([(rq, pair) for pair in range(4)])
-            for step in range(2):
-                if unit >= 4:
-                    out_step()
-        while counts["finished"] < len(out_units):
-            out_step()
+        terms_of[1] = edge_terms(0, 0, 1)
+        transpose_be2()
 
         sums = keep.tile([P, ED], F32)
-        for half in range(OUT_HALVES):
+
+        def finish_sums(half):
             sums_ps = psum_tr.tile([P, 4, P], F32, tag="tr")
             for q in range(4):
                 nc.tensor.transpose(sums_ps[:, q, :], sums_t[:, half * 4 + q, :], ident[:])
-            copy = nc.vector.tensor_copy if half == 0 else nc.scalar.copy
-            copy(out=sums[:, half * BANK : (half + 1) * BANK], in_=sums_ps[:].rearrange("p q f -> p (q f)"))
+            copy = scopy if half == 0 else vcopy
+            copy(
+                out=sums[:, half * BANK : (half + 1) * BANK],
+                in_=sums_ps[:].rearrange("p q f -> p (q f)"),
+            )
+
+        def finish(index):
+            rq, pair = out_list[index]
+            transpose_out(rq, pair, vcopy if False else scopy)
+            if pair % 2 == 1:
+                store(rq, pair - 1, pair + 1)
+
+        def end_of(index):
+            rq, pair = out_list[index]
+            if rq == QUARTERS - 1 and pair % 2 == 1:
+                finish_sums(pair // 2)
+
+        made, finished, summed, late = 0, 0, 0, 0
+        last_piece, x_pending, x_done = [], [], {}
+        beat = 0
+        while late < len(out_list):
+            unit = beat // 2
+            ended = beat % 2 == 0 and 0 < unit <= len(units)
+            if beat < len(beats):
+                g, rq, tp = beats[beat]
+                if tp == 0:
+                    before_relu = sums_h.tile([P, PACK, Q_ROWS], BF16)
+                    before_of[unit] = before_relu
+            if 0 < beat <= len(beats):
+                last_tp = beats[beat - 1][2]
+                add_terms(h_of[beat - 1], last_tp, terms_of[beat - 1], before_of[(beat - 1) // 2])
+            for key in x_pending:
+                quantise_x(*key)
+            x_pending = []
+            for index in last_piece:
+                quantise_piece(index)
+            previous_late, previous, before_sum = late, finished, summed
+            for index in range(summed, made):
+                halve_nodes(*out_list[index])
+            if ended:
+                hidden_of[unit - 1] = relu_hidden(before_of[unit - 1])
+            if beat + 2 < len(beats):
+                ng, nrq, ntp = beats[beat + 2]
+                terms_of[beat + 2] = edge_terms(nrq, ng, ntp)
+            for bank in x_banks.get(beat, []):
+                transpose_x(*bank, scopy)
+                key = bank[:2]
+                x_done[key] = x_done.get(key, 0) + 1
+                if x_done[key] == 2:
+                    x_pending.append(key)
+            last_piece = pieces_at.get(beat, [])
+            for index in last_piece:
+                regroup_piece(index, 4 if index < 8 else 3)
+            for index in range(summed, made):
+                add_up_nodes(*out_list[index])
+            if ended:
+                pg, prq = units[unit - 1]
+                quantise_hidden(prq, pg, hidden_of[unit - 1])
+            for index in range(late, summed):
+                add_to_quarters(*out_list[index])
+            for index in range(summed, made):
+                add_the_halves(*out_list[index])
+            for index in range(finished, made):
+                finish(index)
+            finished = made
+            for index in range(late, summed):
+                end_of(index)
+            late, summed = summed, made
+            for step in range(out_at.get(beat, 0) if beat < len(beats) else 2):
+                if made < len(out_list) and (beat != len(beats) or made < 12):
+                    second_product(*out_list[made])
+                    made += 1
+            if beat < len(beats):
+                h_of[beat] = first_product(rq, g, tp)
+            beat += 1
+
         nc.sync.dma_start(out=out_1, in_=sums[0:NA, :])
         nc.sync.dma_start(out=out_2, in_=sums[NA : NA + NB, :])

@@ -344,14 +344,15 @@ def tile_bipartiteneuralmessagepassinglayer_pa_kernel(
                 so_far = sums_t[:, fts, NA : NA + NB]
                 nc.gpsimd.tensor_tensor(out=so_far, in0=so_far, in1=before, op=ADD)
 
-        def add_the_halves(rq, pair):
+        def halve_again(rq, pair, size):
             if on_gpsimd(rq, pair):
                 return
             tree = halved_of[rq, pair]
-            nc.vector.tensor_reduce(
-                out=tree[:, :, Q_ROWS - NB : Q_ROWS],
-                in_=tree[:, :, 0 : Q_ROWS // 2].rearrange("p f (i j) -> p f j i", j=NB),
-                axis=AXIS_X,
+            first = Q_ROWS - 4 * size
+            nc.vector.tensor_tensor(
+                out=tree[:, :, Q_ROWS - 2 * size : Q_ROWS - size],
+                in0=tree[:, :, first : first + size],
+                in1=tree[:, :, first + size : first + 2 * size],
                 op=ADD,
             )
 
@@ -360,7 +361,7 @@ def tile_bipartiteneuralmessagepassinglayer_pa_kernel(
                 return
             so_far = sums_t[:, 2 * pair : 2 * pair + 2, NA : NA + NB]
             nc.vector.tensor_tensor(
-                out=so_far, in0=so_far, in1=halved_of[rq, pair][:, :, Q_ROWS - NB : Q_ROWS], op=ADD
+                out=so_far, in0=so_far, in1=halved_of[rq, pair][:, :, Q_ROWS - 2 * NB : Q_ROWS - NB], op=ADD
             )
 
         def transpose_out(rq, pair, copy):
@@ -392,19 +393,19 @@ def tile_bipartiteneuralmessagepassinglayer_pa_kernel(
         units = [(0, 0), (0, 1), (1, 0), (1, 1), (0, 2), (1, 2), (0, 3), (1, 3)]
         beats = [(g, rq, tp) for g, rq in units for tp in range(2)]
         x_banks = {}
-        for rq, first, per in [(1, 0, 2), (2, 5, 2), (3, 8, 1)]:
+        for rq, first, per in [(1, 0, 2), (2, 5, 2), (3, 7, 1)]:
             for index in range(4):
                 x_banks.setdefault(first + index // per, []).append((rq, index // 2, index % 2))
         pieces_at = {0: [4], 1: [5, 6], 2: [7], 3: [8], 4: [9], 5: [10], 6: [11]}
         out_at = {8: 1, 9: 1, 10: 1, 11: 2, 12: 1, 13: 1, 14: 2, 15: 1}
         out_list = [(rq, pair) for rq in range(QUARTERS) for pair in range(4)]
 
+        regroup_piece(0, 4)
         transpose_x(0, 0, 0, scopy)
-        regroup_piece(0, 6)
         transpose_x(0, 1, 0, scopy)
-        terms_of[0] = edge_terms(0, 0, 0)
         regroup_piece(1, 6)
         quantise_piece(0)
+        terms_of[0] = edge_terms(0, 0, 0)
         transpose_x(0, 0, 1, scopy)
         regroup_piece(2, 6)
         quantise_piece(1)
@@ -420,14 +421,21 @@ def tile_bipartiteneuralmessagepassinglayer_pa_kernel(
         sums = keep.tile([P, ED], F32)
 
         def finish_sums(half):
-            sums_ps = psum_tr.tile([P, 4, P], F32, tag="tr")
-            for q in range(4):
-                nc.tensor.transpose(sums_ps[:, q, :], sums_t[:, half * 4 + q, :], ident[:])
-            copy = scopy if half == 0 else vcopy
-            copy(
-                out=sums[:, half * BANK : (half + 1) * BANK],
-                in_=sums_ps[:].rearrange("p q f -> p (q f)"),
-            )
+            for part in range(2):
+                sums_ps = psum_tr.tile([P, 2, P], F32, tag="tr")
+                for q in range(2):
+                    nc.tensor.transpose(
+                        sums_ps[:, q, :], sums_t[:, half * 4 + part * 2 + q, :], ident[:]
+                    )
+                first = half * BANK + part * 2 * P
+                copy = scopy if part == 0 else vcopy
+                copy(
+                    out=sums[:, first : first + 2 * P],
+                    in_=sums_ps[:].rearrange("p q f -> p (q f)"),
+                )
+            cols = slice(half * BANK, (half + 1) * BANK)
+            nc.sync.dma_start(out=out_1[:, cols], in_=sums[0:NA, cols])
+            nc.sync.dma_start(out=out_2[:, cols], in_=sums[NA : NA + NB, cols])
 
         def finish(index):
             rq, pair = out_list[index]
@@ -460,8 +468,14 @@ def tile_bipartiteneuralmessagepassinglayer_pa_kernel(
             for index in last_piece:
                 quantise_piece(index)
             previous_late, previous, before_sum = late, finished, summed
-            for index in range(summed, made):
-                halve_nodes(*out_list[index])
+            fresh = [out_list[index] for index in range(summed, made)]
+            for item in fresh:
+                if on_gpsimd(*item):
+                    halve_nodes(*item)
+                    add_up_nodes(*item)
+            for item in fresh:
+                if not on_gpsimd(*item):
+                    halve_nodes(*item)
             if ended:
                 hidden_of[unit - 1] = relu_hidden(before_of[unit - 1])
             if beat + 2 < len(beats):
@@ -476,15 +490,18 @@ def tile_bipartiteneuralmessagepassinglayer_pa_kernel(
             last_piece = pieces_at.get(beat, [])
             for index in last_piece:
                 regroup_piece(index, 4 if index < 8 else 3)
+            for item in fresh:
+                if not on_gpsimd(*item):
+                    add_up_nodes(*item)
             for index in range(summed, made):
-                add_up_nodes(*out_list[index])
+                halve_again(*out_list[index], 2 * NB)
             if ended:
                 pg, prq = units[unit - 1]
                 quantise_hidden(prq, pg, hidden_of[unit - 1])
             for index in range(late, summed):
                 add_to_quarters(*out_list[index])
             for index in range(summed, made):
-                add_the_halves(*out_list[index])
+                halve_again(*out_list[index], NB)
             for index in range(finished, made):
                 finish(index)
             finished = made
@@ -498,6 +515,3 @@ def tile_bipartiteneuralmessagepassinglayer_pa_kernel(
             if beat < len(beats):
                 h_of[beat] = first_product(rq, g, tp)
             beat += 1
-
-        nc.sync.dma_start(out=out_1, in_=sums[0:NA, :])
-        nc.sync.dma_start(out=out_2, in_=sums[NA : NA + NB, :])

@@ -150,10 +150,10 @@ def tile_bipartiteneuralmessagepassinglayer_pa_kernel(
             grouped_of[index] = grouped
             cut = vector_eighths * P // 8
             if index < OUT_HALVES * PASSES_1:
-                dst = grouped[:].rearrange("p (s m t) -> p s m t", s=PACK, t=PACK)
-                src = raw.rearrange("p t (m s) -> p s m t", s=PACK)
+                dst = grouped[:].rearrange("p (s m t) -> p m t s", s=PACK, t=PACK)
+                src = raw.rearrange("p t (m s) -> p m t s", s=PACK)
                 vector_part, scalar_part = (
-                    (slice(None), slice(None), part) for part in (slice(0, cut), slice(cut, P))
+                    (slice(None), part) for part in (slice(0, cut), slice(cut, P))
                 )
             else:
                 dst = grouped[:].rearrange("p (n i t) -> p n t i", i=PACK, t=PACK)

@@ -52,9 +52,9 @@ def tile_bipartiteneuralmessagepassinglayer_pa_kernel(
         latent_pool = ctx.enter_context(tc.tile_pool(name="latent", bufs=5))
         trees = ctx.enter_context(tc.tile_pool(name="trees", bufs=3))
         stores = ctx.enter_context(tc.tile_pool(name="stores", bufs=2))
-        psum_tr = ctx.enter_context(tc.psum_pool(name="psum_tr", bufs=2))
+        psum_tr = ctx.enter_context(tc.psum_pool(name="psum_tr", bufs=3))
         psum_plain = ctx.enter_context(tc.psum_pool(name="psum_plain", bufs=2))
-        psum_mx = ctx.enter_context(tc.psum_pool(name="psum_mx", bufs=4))
+        psum_mx = ctx.enter_context(tc.psum_pool(name="psum_mx", bufs=3))
 
         ctx.enter_context(tc.manual_schedule())
 
@@ -246,7 +246,9 @@ def tile_bipartiteneuralmessagepassinglayer_pa_kernel(
         def relu_hidden(before_relu):
             grouped = hidden.tile([P, Q_ROWS, PACK], BF16, align_bytes=64)
             nc.vector.tensor_scalar_max(
-                out=grouped[:], in0=before_relu[:].rearrange("p t r -> p r t"), scalar1=0.0
+                out=grouped[:].rearrange("p (r i) t -> p r t i", i=PACK),
+                in0=before_relu[:].rearrange("p t (r i) -> p r t i", i=PACK),
+                scalar1=0.0,
             )
             return grouped
 

@@ -21,16 +21,20 @@ NA, NB = 32, 32
 ROWS = NA * NB
 K1 = 2048
 ED = 1024
-ROW_TILES = ROWS // P
-A_PER_TILE = P // NB
 PASSES_1 = K1 // K_PASS
 PASSES_2 = ED // K_PASS
-OUT_HALVES = ED // BANK
+HALVES = ED // BANK
 OUT_TILES = ED // P
-Q_ROWS = 2 * P
-QUARTERS = ROWS // Q_ROWS
-A_PER_QUARTER = Q_ROWS // NB
-BE1_ROW, BE2_ROW = 64, 96
+
+GROUP = 256
+GROUPS = ROWS // GROUP
+TILES = GROUP // P
+SLOTS = BANK // GROUP
+GROUP_NA = GROUP // NB
+PARTS_1 = PACK // SLOTS
+PARTS_2 = OUT_TILES // SLOTS
+
+BE1_ROW, BE2_ROW = NA + NB, 96
 
 FLOPS = 2 * ROWS * K1 * ED + 2 * ROWS * ED * ED
 
@@ -47,7 +51,7 @@ def tile_bipartiteneuralmessagepassinglayer_pa_kernel(
         grouped_w = ctx.enter_context(tc.tile_pool(name="grouped_w", bufs=3))
         grouped_x = ctx.enter_context(tc.tile_pool(name="grouped_x", bufs=4))
         terms_pool = ctx.enter_context(tc.tile_pool(name="terms", bufs=4))
-        sums_h = ctx.enter_context(tc.tile_pool(name="sums_h", bufs=2))
+        before_relu = ctx.enter_context(tc.tile_pool(name="before_relu", bufs=2))
         hidden = ctx.enter_context(tc.tile_pool(name="hidden", bufs=3))
         latent_pool = ctx.enter_context(tc.tile_pool(name="latent", bufs=5))
         trees = ctx.enter_context(tc.tile_pool(name="trees", bufs=3))
@@ -59,11 +63,11 @@ def tile_bipartiteneuralmessagepassinglayer_pa_kernel(
         ctx.enter_context(tc.manual_schedule())
 
         node_rows = keep.tile([P, ED], BF16)
-        we_raw = keep.tile([P, OUT_HALVES, PASSES_1, PACK, BANK], BF16)
+        we_raw = keep.tile([P, HALVES, PASSES_1, PACK, BANK], BF16)
         we2_raw = keep.tile([P, PASSES_2, PACK, ED], BF16)
-        x_raw = keep.tile([P, ROW_TILES * K1], BF16)
+        x_raw = keep.tile([P, ROWS // P, K1], BF16)
 
-        def load_we_piece(half, c):
+        def load_we(half, c):
             nc.sync.dma_start(
                 out=we_raw[:, half, c],
                 in_=We[
@@ -71,37 +75,35 @@ def tile_bipartiteneuralmessagepassinglayer_pa_kernel(
                 ].rearrange("(p t) n -> p t n", t=PACK),
             )
 
-        def load_x(rt):
+        def load_we2(g):
             nc.sync.dma_start(
-                out=x_raw[:, rt * K1 : (rt + 1) * K1], in_=x_rows[rt * P : (rt + 1) * P, :]
+                out=we2_raw[:, g],
+                in_=We2[g * K_PASS : (g + 1) * K_PASS, :].rearrange("(p t) n -> p t n", t=PACK),
             )
 
-        load_we_piece(0, 0)
+        def load_x(rt):
+            nc.sync.dma_start(out=x_raw[:, rt], in_=x_rows[rt * P : (rt + 1) * P, :])
+
+        load_we(0, 0)
         load_x(0)
         nc.sync.dma_start(out=node_rows[0:NA, :], in_=a_proj)
         nc.sync.dma_start(out=node_rows[NA : NA + NB, :], in_=b_proj)
-        nc.sync.dma_start(out=node_rows[BE1_ROW:BE2_ROW, :], in_=be1.partition_broadcast(BE2_ROW - BE1_ROW))
+        nc.sync.dma_start(
+            out=node_rows[BE1_ROW:BE2_ROW, :], in_=be1.partition_broadcast(BE2_ROW - BE1_ROW)
+        )
         nc.sync.dma_start(out=node_rows[BE2_ROW:P, :], in_=be2.partition_broadcast(P - BE2_ROW))
-        load_we_piece(0, 1)
+        load_we(0, 1)
         load_x(1)
-        load_we_piece(0, 2)
-        load_we_piece(0, 3)
+        load_we(0, 2)
+        load_we(0, 3)
         load_x(2)
         load_x(3)
-        load_we_piece(1, 0)
-        load_we_piece(1, 1)
-        load_we_piece(1, 2)
-        load_we_piece(1, 3)
+        for c in range(PASSES_1):
+            load_we(1, c)
+        load_we2(0)
         load_x(4)
-        nc.sync.dma_start(
-            out=we2_raw[:, 0],
-            in_=We2[0 * K_PASS : 1 * K_PASS, :].rearrange("(p t) n -> p t n", t=PACK),
-        )
         load_x(5)
-        nc.sync.dma_start(
-            out=we2_raw[:, 1],
-            in_=We2[1 * K_PASS : 2 * K_PASS, :].rearrange("(p t) n -> p t n", t=PACK),
-        )
+        load_we2(1)
         load_x(6)
         load_x(7)
 
@@ -111,7 +113,6 @@ def tile_bipartiteneuralmessagepassinglayer_pa_kernel(
         masks.make_identity(nc, ident[:])
         table_warmer = keep.tile([P, 1], F32)
         nc.scalar.activation(out=table_warmer[:], in_=ident[:, 0:1], func=RELU)
-
         ident_bf = keep.tile([P, P], BF16)
         nc.vector.tensor_copy(out=ident_bf[:], in_=ident[:])
         pick = keep.tile([P, NA, NB], BF16)
@@ -122,9 +123,10 @@ def tile_bipartiteneuralmessagepassinglayer_pa_kernel(
             op=ADD,
         )
         nc.vector.tensor_scalar_add(
-            out=pick[:], in0=pick[:], scalar1=ident[:, NA + NB : NA + NB + 1]
+            out=pick[:], in0=pick[:], scalar1=ident[:, BE1_ROW : BE1_ROW + 1]
         )
         pick_cols = pick[:].rearrange("k i j -> k (i j)")
+
         we_codes = keep.tile([P, PASSES_1 * ED], U32, align_bytes=64)
         we_scales = keep.tile([P, PASSES_1 * ED], U8, align_bytes=64)
         we2_codes = keep.tile([P, PASSES_2 * ED], U32, align_bytes=64)
@@ -135,11 +137,12 @@ def tile_bipartiteneuralmessagepassinglayer_pa_kernel(
         h_scales = keep.tile([P, PASSES_2 * ROWS], U8, align_bytes=64)
 
         pieces = []
-        for half in range(OUT_HALVES):
+        for half in range(HALVES):
             for c in range(PASSES_1):
                 pieces.append((we_raw[:, half, c], we_codes, we_scales, c * ED + half * BANK))
+        first_we2_piece = len(pieces)
         for g in range(PASSES_2):
-            for half in range(OUT_HALVES):
+            for half in range(HALVES):
                 cols = slice(half * BANK, (half + 1) * BANK)
                 pieces.append((we2_raw[:, g, :, cols], we2_codes, we2_scales, g * ED + half * BANK))
         grouped_of = {}
@@ -148,87 +151,78 @@ def tile_bipartiteneuralmessagepassinglayer_pa_kernel(
             raw = pieces[index][0]
             grouped = grouped_w.tile([P, BANK * PACK], BF16, align_bytes=64)
             grouped_of[index] = grouped
-            cut = vector_eighths * P // 8
-            if index < OUT_HALVES * PASSES_1:
+            if index < first_we2_piece:
                 dst = grouped[:].rearrange("p (s m t) -> p m t s", s=PACK, t=PACK)
-                src = raw.rearrange("p t (m s) -> p m t s", s=PACK)
-                vector_part, scalar_part = (
-                    (slice(None), part) for part in (slice(0, cut), slice(cut, P))
-                )
             else:
-                dst = grouped[:].rearrange("p (n i t) -> p n t i", i=PACK, t=PACK)
-                src = raw.rearrange("p t (n i) -> p n t i", i=PACK)
-                vector_part, scalar_part = (
-                    (slice(None), part) for part in (slice(0, cut), slice(cut, P))
-                )
-            if cut > 0:
-                nc.vector.tensor_copy(out=dst[vector_part], in_=src[vector_part])
-            if cut < P:
-                nc.scalar.copy(out=dst[scalar_part], in_=src[scalar_part])
+                dst = grouped[:].rearrange("p (m s t) -> p m t s", s=PACK, t=PACK)
+            src = raw.rearrange("p t (m s) -> p m t s", s=PACK)
+            cut = vector_eighths * P // 8
+            nc.vector.tensor_copy(out=dst[:, :cut], in_=src[:, :cut])
+            nc.scalar.copy(out=dst[:, cut:], in_=src[:, cut:])
 
         def quantise_piece(index):
             codes, scales, first_col = pieces[index][1:]
             cols = slice(first_col, first_col + BANK)
             nc.vector.quantize_mx(
-                out=codes[:, cols].bitcast(FP8X4),
-                scales=scales[:, cols],
-                in_=grouped_of[index][:],
+                out=codes[:, cols].bitcast(FP8X4), scales=scales[:, cols], in_=grouped_of[index][:]
             )
 
-        x_words = x_raw[:].bitcast(F32)
-        words_per_row = K1 // 2
+        grouped_x_of = {}
 
-        grouped_of_x = {}
-
-        def transpose_x(rq, pair, q, copy):
-            if (rq, pair) not in grouped_of_x:
-                grouped = grouped_x.tile([P, 2 * Q_ROWS * PACK], BF16, align_bytes=64)
-                grouped_of_x[rq, pair] = grouped
-            grouped_words = grouped_of_x[rq, pair][:].bitcast(F32).rearrange(
-                "p (c q r u) -> p q c r u", c=2, q=2, u=2
-            )
-            first_word = (2 * rq + q) * words_per_row
+        def transpose_x(group, pair, q):
+            if (group, pair) not in grouped_x_of:
+                grouped = grouped_x.tile([P, 2 * GROUP * PACK], BF16, align_bytes=64)
+                grouped_x_of[group, pair] = grouped
+            words = x_raw[:, group * TILES + q].bitcast(F32)
             xt = psum_tr.tile([P, 4, P], F32, tag="tr")
-            for quarter in range(4):
-                c, u = divmod(pair * 4 + quarter, 2)
-                first = first_word + c * 2 * P
+            for index in range(4):
+                c, u = divmod(pair * 4 + index, 2)
+                first = c * 2 * P
                 nc.tensor.transpose(
-                    xt[:, quarter, :], x_words[:, first + u : first + 2 * P : 2], ident[:]
+                    xt[:, index, :], words[:, first + u : first + 2 * P : 2], ident[:]
                 )
-            copy(out=grouped_words[:, q], in_=xt[:].rearrange("p (c u) r -> p c r u", u=2))
-
-        def quantise_x(rq, pair):
-            first = (rq * PASSES_1 + 2 * pair) * Q_ROWS
-            cols = slice(first, first + 2 * Q_ROWS)
-            nc.vector.quantize_mx(
-                out=x_codes[:, cols].bitcast(FP8X4), scales=x_scales[:, cols], in_=grouped_of_x[rq, pair][:]
+            grouped_words = grouped_x_of[group, pair][:].bitcast(F32)
+            nc.scalar.copy(
+                out=grouped_words.rearrange("p (c q r u) -> p q c r u", c=2, r=P, u=2)[:, q],
+                in_=xt[:].rearrange("p (c u) r -> p c r u", u=2),
             )
 
-        def edge_terms(rq, g, tp):
-            terms_ps = psum_plain.tile([P, 2, Q_ROWS], F32, tag="plain")
-            for t in range(2):
-                first = g * K_PASS + 2 * tp + t
+        def x_columns(group, c, passes):
+            first = (group * PASSES_1 + c) * GROUP
+            return slice(first, first + passes * GROUP)
+
+        def quantise_x(group, pair):
+            cols = x_columns(group, 2 * pair, 2)
+            nc.vector.quantize_mx(
+                out=x_codes[:, cols].bitcast(FP8X4),
+                scales=x_scales[:, cols],
+                in_=grouped_x_of[group, pair][:],
+            )
+
+        def edge_terms(group, g, part):
+            terms_ps = psum_plain.tile([P, SLOTS, GROUP], F32, tag="plain")
+            for slot in range(SLOTS):
+                first = g * K_PASS + part * SLOTS + slot
                 nc.tensor.matmul(
-                    terms_ps[:, t, :],
+                    terms_ps[:, slot, :],
                     lhsT=node_rows[:, first : (g + 1) * K_PASS : PACK],
-                    rhs=pick_cols[:, rq * Q_ROWS : (rq + 1) * Q_ROWS],
+                    rhs=pick_cols[:, group * GROUP : (group + 1) * GROUP],
                     start=True,
                     stop=True,
                 )
-            terms = terms_pool.tile([P, 2, Q_ROWS], F32)
+            terms = terms_pool.tile([P, SLOTS, GROUP], F32)
             nc.scalar.copy(out=terms[:], in_=terms_ps[:])
             return terms
 
-        def first_product(rq, g, tp):
-            h_ps = psum_mx.tile([P, 2, Q_ROWS], F32, tag="mx")
-            for t in range(2):
-                e_tile = g * PACK + 2 * tp + t
+        def first_product(group, g, part):
+            h_ps = psum_mx.tile([P, SLOTS, GROUP], F32, tag="mx")
+            for slot in range(SLOTS):
+                first_col = g * BANK + (part * SLOTS + slot) * P
                 for c in range(PASSES_1):
-                    w_cols = slice(c * ED + e_tile * P, c * ED + (e_tile + 1) * P)
-                    first = (rq * PASSES_1 + c) * Q_ROWS
-                    r_cols = slice(first, first + Q_ROWS)
+                    w_cols = slice(c * ED + first_col, c * ED + first_col + P)
+                    r_cols = x_columns(group, c, 1)
                     nc.tensor.matmul_mx(
-                        out=h_ps[:, t, :],
+                        out=h_ps[:, slot, :],
                         lhsT=we_codes[:, w_cols].bitcast(FP8X4),
                         lhsT_scale=we_scales[:, w_cols],
                         rhs=x_codes[:, r_cols].bitcast(FP8X4),
@@ -238,22 +232,25 @@ def tile_bipartiteneuralmessagepassinglayer_pa_kernel(
                     )
             return h_ps
 
-        def add_terms(h_ps, tp, terms, before_relu):
-            nc.vector.tensor_tensor(
-                out=before_relu[:, 2 * tp : 2 * tp + 2, :], in0=h_ps[:], in1=terms[:], op=ADD
-            )
+        def add_terms(part, h_ps, terms, sums_h):
+            slots = slice(part * SLOTS, (part + 1) * SLOTS)
+            nc.vector.tensor_tensor(out=sums_h[:, slots, :], in0=h_ps[:], in1=terms[:], op=ADD)
 
-        def relu_hidden(before_relu):
-            grouped = hidden.tile([P, Q_ROWS, PACK], BF16, align_bytes=64)
+        def relu_hidden(sums_h):
+            grouped = hidden.tile([P, GROUP, PACK], BF16, align_bytes=64)
             nc.vector.tensor_scalar_max(
                 out=grouped[:].rearrange("p (r i) t -> p r t i", i=PACK),
-                in0=before_relu[:].rearrange("p t (r i) -> p r t i", i=PACK),
+                in0=sums_h[:].rearrange("p t (r i) -> p r t i", i=PACK),
                 scalar1=0.0,
             )
             return grouped
 
-        def quantise_hidden(rq, g, grouped):
-            cols = slice(g * ROWS + rq * Q_ROWS, g * ROWS + (rq + 1) * Q_ROWS)
+        def h_columns(g, group):
+            first = g * ROWS + group * GROUP
+            return slice(first, first + GROUP)
+
+        def quantise_hidden(group, g, grouped):
+            cols = h_columns(g, group)
             nc.vector.quantize_mx(
                 out=h_codes[:, cols].bitcast(FP8X4),
                 scales=h_scales[:, cols],
@@ -274,17 +271,19 @@ def tile_bipartiteneuralmessagepassinglayer_pa_kernel(
                 )
             nc.scalar.copy(out=be2_cols[:], in_=be2_ps[:, :, 0])
 
-        latent_of, natural_of = {}, {}
+        latent_of, natural_of, tree_of = {}, {}, {}
 
-        def second_product(rq, pair):
-            o_ps = psum_mx.tile([P, 2, Q_ROWS], F32, tag="mx")
-            for half in range(2):
-                ft = 2 * pair + half
+        def second_product(group, part):
+            o_ps = psum_mx.tile([P, SLOTS, GROUP], F32, tag="mx")
+            latent = latent_pool.tile([P, SLOTS, GROUP], F32)
+            latent_of[group, part] = latent
+            for slot in range(SLOTS):
+                first_col = (part * SLOTS + slot) * P
                 for g in range(PASSES_2):
-                    r_cols = slice(g * ROWS + rq * Q_ROWS, g * ROWS + (rq + 1) * Q_ROWS)
-                    f_cols = slice(g * ED + ft * P, g * ED + (ft + 1) * P)
+                    f_cols = slice(g * ED + first_col, g * ED + first_col + P)
+                    r_cols = h_columns(g, group)
                     nc.tensor.matmul_mx(
-                        out=o_ps[:, half, :],
+                        out=o_ps[:, slot, :],
                         lhsT=we2_codes[:, f_cols].bitcast(FP8X4),
                         lhsT_scale=we2_scales[:, f_cols],
                         rhs=h_codes[:, r_cols].bitcast(FP8X4),
@@ -292,145 +291,87 @@ def tile_bipartiteneuralmessagepassinglayer_pa_kernel(
                         start=(g == 0),
                         stop=(g == PASSES_2 - 1),
                     )
-            latent = latent_pool.tile([P, 2, Q_ROWS], F32)
-            latent_of[rq, pair] = latent
-            for half in range(2):
-                ft = 2 * pair + half
+            for slot in range(SLOTS):
+                ft = part * SLOTS + slot
                 nc.scalar.activation(
-                    out=latent[:, half, :],
-                    in_=o_ps[:, half, :],
+                    out=latent[:, slot, :],
+                    in_=o_ps[:, slot, :],
                     func=RELU,
                     bias=be2_cols[:, ft : ft + 1],
                 )
 
-        def on_gpsimd(rq, pair):
-            return pair % 2 == 0
+        def on_gpsimd(group, part):
+            return part % 2 == 0
 
-        def add_up_nodes(rq, pair):
-            latent = latent_of[rq, pair]
+        def out_tiles(part):
+            return slice(part * SLOTS, (part + 1) * SLOTS)
+
+        def start_tree(group, part):
+            tree = trees.tile([P, SLOTS, GROUP], F32)
+            tree_of[group, part] = tree
+
+        def add_up_b_nodes(group, part):
             nc.vector.tensor_reduce(
-                out=sums_t[:, 2 * pair : 2 * pair + 2, rq * A_PER_QUARTER : (rq + 1) * A_PER_QUARTER],
-                in_=latent[:].rearrange("p f (i j) -> p f i j", j=NB),
+                out=sums_t[:, out_tiles(part), group * GROUP_NA : (group + 1) * GROUP_NA],
+                in_=latent_of[group, part][:].rearrange("p f (i j) -> p f i j", j=NB),
                 axis=AXIS_X,
                 op=ADD,
             )
 
-        halved_of = {}
+        def sum_b_of(part):
+            return sums_t[:, out_tiles(part), NA : NA + NB]
 
-        def halve_nodes(rq, pair):
-            latent = latent_of[rq, pair]
-            tree = trees.tile([P, 2, Q_ROWS], F32)
-            halved_of[rq, pair] = tree
-            fts = slice(2 * pair, 2 * pair + 2)
-            if not on_gpsimd(rq, pair):
-                nc.vector.tensor_tensor(
-                    out=tree[:, :, 0 : Q_ROWS // 2],
-                    in0=latent[:, :, 0 : Q_ROWS // 2],
-                    in1=latent[:, :, Q_ROWS // 2 : Q_ROWS],
-                    op=ADD,
-                )
-                return
-            size = Q_ROWS // 2
-            before = latent[:]
-            while size >= NB:
-                if size == NB and rq == 0:
-                    after = sums_t[:, fts, NA : NA + NB]
-                else:
-                    after = tree[:, :, Q_ROWS - 2 * size : Q_ROWS - size]
-                nc.gpsimd.tensor_tensor(
-                    out=after, in0=before[:, :, 0:size], in1=before[:, :, size : 2 * size], op=ADD
-                )
-                before = after
-                size //= 2
-            if rq > 0:
-                so_far = sums_t[:, fts, NA : NA + NB]
-                nc.gpsimd.tensor_tensor(out=so_far, in0=so_far, in1=before, op=ADD)
-
-        def halve_again(rq, pair, size):
-            if on_gpsimd(rq, pair):
-                return
-            tree = halved_of[rq, pair]
-            first = Q_ROWS - 4 * size
-            nc.vector.tensor_tensor(
-                out=tree[:, :, Q_ROWS - 2 * size : Q_ROWS - size],
-                in0=tree[:, :, first : first + size],
-                in1=tree[:, :, first + size : first + 2 * size],
+        def halve(engine, group, part, step, out=None):
+            left = GROUP >> step
+            tree = tree_of[group, part]
+            source, first = (tree, GROUP - 2 * left) if step > 0 else (latent_of[group, part], 0)
+            engine.tensor_tensor(
+                out=tree[:, :, GROUP - left : GROUP - left // 2] if out is None else out,
+                in0=source[:, :, first : first + left // 2],
+                in1=source[:, :, first + left // 2 : first + left],
                 op=ADD,
             )
 
-        def add_to_quarters(rq, pair):
-            if on_gpsimd(rq, pair):
-                return
-            so_far = sums_t[:, 2 * pair : 2 * pair + 2, NA : NA + NB]
-            nc.vector.tensor_tensor(
-                out=so_far, in0=so_far, in1=halved_of[rq, pair][:, :, Q_ROWS - 2 * NB : Q_ROWS - NB], op=ADD
-            )
+        def add_to_sum_b(engine, group, part):
+            so_far = sum_b_of(part)
+            group_sum = tree_of[group, part][:, :, GROUP - 2 * NB : GROUP - NB]
+            engine.tensor_tensor(out=so_far, in0=so_far, in1=group_sum, op=ADD)
 
-        def transpose_out(rq, pair, copy):
-            if pair == 0:
-                natural = stores.tile([P, 2, ED], F32)
-                natural_of[rq] = natural
-            rows_ps = psum_tr.tile([P, 2, 2, P], F32, tag="tr")
-            for half in range(2):
-                for q in range(2):
+        def transpose_out(group, part):
+            if part == 0:
+                natural = stores.tile([P, TILES, ED], F32)
+                natural_of[group] = natural
+            rows_ps = psum_tr.tile([P, TILES, SLOTS, P], F32, tag="tr")
+            for slot in range(SLOTS):
+                for q in range(TILES):
                     nc.tensor.transpose(
-                        rows_ps[:, q, half, :],
-                        latent_of[rq, pair][:, half, q * P : (q + 1) * P],
+                        rows_ps[:, q, slot, :],
+                        latent_of[group, part][:, slot, q * P : (q + 1) * P],
                         ident[:],
                     )
-            copy(
-                out=natural_of[rq][:, :, 2 * pair * P : 2 * (pair + 1) * P],
+            last_col = (part + 1) * SLOTS * P
+            nc.scalar.copy(
+                out=natural_of[group][:, :, last_col - SLOTS * P : last_col],
                 in_=rows_ps[:].rearrange("p q f r -> p q (f r)"),
             )
-
-        def store(rq, first, last):
-            cols = slice(2 * first * P, 2 * last * P)
-            nc.sync.dma_start(
-                out=latent_rows[rq * Q_ROWS : (rq + 1) * Q_ROWS, cols].rearrange("(q p) f -> p q f", p=P),
-                in_=natural_of[rq][:, :, cols],
-            )
-
-        vcopy, scopy = nc.vector.tensor_copy, nc.scalar.copy
-        terms_of, h_of, before_of, hidden_of = {}, {}, {}, {}
-        units = [(0, 0), (0, 1), (1, 0), (1, 1), (0, 2), (1, 2), (0, 3), (1, 3)]
-        beats = [(g, rq, tp) for g, rq in units for tp in range(2)]
-        x_banks = {}
-        for rq, first, per in [(1, 0, 2), (2, 5, 2), (3, 7, 1)]:
-            for index in range(4):
-                x_banks.setdefault(first + index // per, []).append((rq, index // 2, index % 2))
-        pieces_at = {0: [4], 1: [5, 6], 2: [7], 3: [8], 4: [9], 5: [10], 6: [11]}
-        out_at = {8: 1, 9: 1, 10: 1, 11: 2, 12: 1, 13: 1, 14: 2, 15: 1}
-        out_list = [(rq, pair) for rq in range(QUARTERS) for pair in range(4)]
-
-        regroup_piece(0, 4)
-        transpose_x(0, 0, 0, scopy)
-        transpose_x(0, 1, 0, scopy)
-        regroup_piece(1, 6)
-        quantise_piece(0)
-        terms_of[0] = edge_terms(0, 0, 0)
-        transpose_x(0, 0, 1, scopy)
-        regroup_piece(2, 6)
-        quantise_piece(1)
-        transpose_x(0, 1, 1, scopy)
-        quantise_x(0, 0)
-        regroup_piece(3, 6)
-        quantise_piece(2)
-        quantise_x(0, 1)
-        quantise_piece(3)
-        terms_of[1] = edge_terms(0, 0, 1)
-        transpose_be2()
+            if last_col % BANK == 0:
+                cols = slice(last_col - BANK, last_col)
+                nc.sync.dma_start(
+                    out=latent_rows[group * GROUP : (group + 1) * GROUP, cols].rearrange(
+                        "(q p) f -> p q f", p=P
+                    ),
+                    in_=natural_of[group][:, :, cols],
+                )
 
         sums = keep.tile([P, ED], F32)
 
         def finish_sums(half):
-            for part in range(2):
+            for quarter in range(2):
+                first = half * BANK + quarter * 2 * P
                 sums_ps = psum_tr.tile([P, 2, P], F32, tag="tr")
                 for q in range(2):
-                    nc.tensor.transpose(
-                        sums_ps[:, q, :], sums_t[:, half * 4 + part * 2 + q, :], ident[:]
-                    )
-                first = half * BANK + part * 2 * P
-                copy = scopy if part == 0 else vcopy
+                    nc.tensor.transpose(sums_ps[:, q, :], sums_t[:, first // P + q, :], ident[:])
+                copy = nc.scalar.copy if quarter == 0 else nc.vector.tensor_copy
                 copy(
                     out=sums[:, first : first + 2 * P],
                     in_=sums_ps[:].rearrange("p q f -> p (q f)"),
@@ -439,81 +380,121 @@ def tile_bipartiteneuralmessagepassinglayer_pa_kernel(
             nc.sync.dma_start(out=out_1[:, cols], in_=sums[0:NA, cols])
             nc.sync.dma_start(out=out_2[:, cols], in_=sums[NA : NA + NB, cols])
 
-        def finish(index):
-            rq, pair = out_list[index]
-            transpose_out(rq, pair, vcopy if False else scopy)
-            if pair % 2 == 1:
-                store(rq, pair - 1, pair + 1)
+        units = [(g, group) for g in range(PASSES_2) for group in (0, 1)]
+        units += [(g, group) for group in (2, 3) for g in range(PASSES_2)]
+        beats = [(g, group, part) for g, group in units for part in range(PARTS_1)]
+        outs = [(group, part) for group in range(GROUPS) for part in range(PARTS_2)]
+        C_BEAT = 8
 
-        def end_of(index):
-            rq, pair = out_list[index]
-            if rq == QUARTERS - 1 and pair % 2 == 1:
-                finish_sums(pair // 2)
+        def pieces_in(beat):
+            return [index for index in range(4, len(pieces)) if beat == index - (4 if index < 6 else 5)]
 
-        made, finished, summed, late = 0, 0, 0, 0
-        last_piece, x_pending, x_done = [], [], {}
+        x_first = {1: (0, 2), 2: (5, 2), 3: (7, 1)}
+
+        def x_banks_in(beat):
+            return [
+                (group, index // TILES, index % TILES)
+                for group, (first, per_beat) in x_first.items()
+                for index in range(2 * TILES)
+                if beat == first + index // per_beat
+            ]
+
+        def outs_in(beat):
+            if beat < C_BEAT:
+                return 0
+            if beat < len(beats):
+                return 2 if beat > C_BEAT and beat % 3 == 2 else 1
+            return 2
+
+        regroup_piece(0, 4)
+        transpose_x(0, 0, 0)
+        transpose_x(0, 1, 0)
+        regroup_piece(1, 6)
+        quantise_piece(0)
+        terms_of = {0: edge_terms(0, 0, 0)}
+        transpose_x(0, 0, 1)
+        regroup_piece(2, 6)
+        quantise_piece(1)
+        transpose_x(0, 1, 1)
+        quantise_x(0, 0)
+        regroup_piece(3, 6)
+        quantise_piece(2)
+        quantise_x(0, 1)
+        quantise_piece(3)
+        terms_of[1] = edge_terms(0, 0, 1)
+        transpose_be2()
+
+        h_of, sums_h_of = {}, {}
+        made, summed, added = 0, 0, 0
+        x_ready, pieces_ready = [], []
         beat = 0
-        while late < len(out_list):
-            unit = beat // 2
-            ended = beat % 2 == 0 and 0 < unit <= len(units)
-            if beat < len(beats):
-                g, rq, tp = beats[beat]
-                if tp == 0:
-                    before_relu = sums_h.tile([P, PACK, Q_ROWS], BF16)
-                    before_of[unit] = before_relu
+        while added < len(outs):
             if 0 < beat <= len(beats):
-                last_tp = beats[beat - 1][2]
-                add_terms(h_of[beat - 1], last_tp, terms_of[beat - 1], before_of[(beat - 1) // 2])
-            for key in x_pending:
-                quantise_x(*key)
-            x_pending = []
-            for index in last_piece:
+                part = beats[beat - 1][2]
+                add_terms(part, h_of[beat - 1], terms_of[beat - 1], sums_h_of[(beat - 1) // PARTS_1])
+            for group, pair in x_ready:
+                quantise_x(group, pair)
+            for index in pieces_ready:
                 quantise_piece(index)
-            previous_late, previous, before_sum = late, finished, summed
-            fresh = [out_list[index] for index in range(summed, made)]
-            for item in fresh:
-                if on_gpsimd(*item):
-                    halve_nodes(*item)
-                    add_up_nodes(*item)
-            for item in fresh:
-                if not on_gpsimd(*item):
-                    halve_nodes(*item)
-            if ended:
-                hidden_of[unit - 1] = relu_hidden(before_of[unit - 1])
+
+            fresh = outs[summed:made]
+            for_gpsimd = [item for item in fresh if on_gpsimd(*item)]
+            for_vector = [item for item in fresh if not on_gpsimd(*item)]
+            for group, part in for_gpsimd:
+                start_tree(group, part)
+                halve(nc.gpsimd, group, part, 0)
+                halve(nc.gpsimd, group, part, 1)
+                if group == 0:
+                    halve(nc.gpsimd, group, part, 2, out=sum_b_of(part))
+                else:
+                    halve(nc.gpsimd, group, part, 2)
+                    add_to_sum_b(nc.gpsimd, group, part)
+                add_up_b_nodes(group, part)
+            for group, part in for_vector:
+                start_tree(group, part)
+                halve(nc.vector, group, part, 0)
+            unit_ended = beat % PARTS_1 == 0 and 0 < beat <= len(beats)
+            if unit_ended:
+                grouped_h = relu_hidden(sums_h_of[beat // PARTS_1 - 1])
             if beat + 2 < len(beats):
-                ng, nrq, ntp = beats[beat + 2]
-                terms_of[beat + 2] = edge_terms(nrq, ng, ntp)
-            for bank in x_banks.get(beat, []):
-                transpose_x(*bank, scopy)
-                key = bank[:2]
-                x_done[key] = x_done.get(key, 0) + 1
-                if x_done[key] == 2:
-                    x_pending.append(key)
-            last_piece = pieces_at.get(beat, [])
-            for index in last_piece:
-                regroup_piece(index, 4 if index < 8 else 3)
-            for item in fresh:
-                if not on_gpsimd(*item):
-                    add_up_nodes(*item)
-            for index in range(summed, made):
-                halve_again(*out_list[index], 2 * NB)
-            if ended:
-                pg, prq = units[unit - 1]
-                quantise_hidden(prq, pg, hidden_of[unit - 1])
-            for index in range(late, summed):
-                add_to_quarters(*out_list[index])
-            for index in range(summed, made):
-                halve_again(*out_list[index], NB)
-            for index in range(finished, made):
-                finish(index)
-            finished = made
-            for index in range(late, summed):
-                end_of(index)
-            late, summed = summed, made
-            for step in range(out_at.get(beat, 0) if beat < len(beats) else 2):
-                if made < len(out_list) and (beat != len(beats) or made < 12):
-                    second_product(*out_list[made])
+                g, group, part = beats[beat + 2]
+                terms_of[beat + 2] = edge_terms(group, g, part)
+            x_ready = []
+            for group, pair, q in x_banks_in(beat):
+                transpose_x(group, pair, q)
+                if q == TILES - 1:
+                    x_ready.append((group, pair))
+            pieces_ready = pieces_in(beat)
+            for index in pieces_ready:
+                regroup_piece(index, 4 if index < first_we2_piece else 3)
+            for group, part in for_vector:
+                add_up_b_nodes(group, part)
+            for group, part in for_vector:
+                halve(nc.vector, group, part, 1)
+            if unit_ended:
+                g, group = units[beat // PARTS_1 - 1]
+                quantise_hidden(group, g, grouped_h)
+            for group, part in outs[added:summed]:
+                if not on_gpsimd(group, part):
+                    add_to_sum_b(nc.vector, group, part)
+            for group, part in for_vector:
+                halve(nc.vector, group, part, 2)
+
+            for group, part in fresh:
+                transpose_out(group, part)
+            for group, part in outs[added:summed]:
+                if group == GROUPS - 1 and part % 2 == 1:
+                    finish_sums(part // 2)
+            added, summed = summed, made
+            for group, part in outs[made : made + outs_in(beat)]:
+                if beat > len(beats) or group < GROUPS - 1:
+                    second_product(group, part)
                     made += 1
+
             if beat < len(beats):
-                h_of[beat] = first_product(rq, g, tp)
+                g, group, part = beats[beat]
+                if part == 0:
+                    sums_h = before_relu.tile([P, PACK, GROUP], BF16)
+                    sums_h_of[beat // PARTS_1] = sums_h
+                h_of[beat] = first_product(group, g, part)
             beat += 1

from contextlib import ExitStack

import concourse.masks as masks
import concourse.mybir as mybir

F32 = mybir.dt.float32
BF16 = mybir.dt.bfloat16
U32 = mybir.dt.uint32
U8 = mybir.dt.uint8
FP8X4 = mybir.dt.float8_e4m3fn_x4
ADD = mybir.AluOpType.add
RELU = mybir.ActivationFunctionType.Relu
AXIS_X = mybir.AxisListType.X

P = 128
PACK = 4
K_PASS = P * PACK
BANK = 512

NA, NB = 32, 32
ROWS = NA * NB
K1 = 2048
ED = 1024
PASSES_1 = K1 // K_PASS
PASSES_2 = ED // K_PASS
HALVES = ED // BANK
OUT_TILES = ED // P

GROUP = 256
GROUPS = ROWS // GROUP
TILES = GROUP // P
SLOTS = BANK // GROUP
GROUP_NA = GROUP // NB
PARTS_1 = PACK // SLOTS
PARTS_2 = OUT_TILES // SLOTS

BE1_ROW, BE2_ROW = NA + NB, 96

FLOPS = 2 * ROWS * K1 * ED + 2 * ROWS * ED * ED


def tile_bipartiteneuralmessagepassinglayer_pa_kernel(
    tc, edge_embeds, a_proj, b_proj, We, be1, We2, be2, out_0, out_1, out_2
):
    nc = tc.nc
    x_rows = edge_embeds.rearrange("a b k -> (a b) k")
    latent_rows = out_0.rearrange("a b f -> (a b) f")

    with ExitStack() as ctx:
        keep = ctx.enter_context(tc.tile_pool(name="keep", bufs=1))
        grouped_w = ctx.enter_context(tc.tile_pool(name="grouped_w", bufs=3))
        grouped_x = ctx.enter_context(tc.tile_pool(name="grouped_x", bufs=4))
        terms_pool = ctx.enter_context(tc.tile_pool(name="terms", bufs=4))
        before_relu = ctx.enter_context(tc.tile_pool(name="before_relu", bufs=2))
        hidden = ctx.enter_context(tc.tile_pool(name="hidden", bufs=3))
        latent_pool = ctx.enter_context(tc.tile_pool(name="latent", bufs=5))
        trees = ctx.enter_context(tc.tile_pool(name="trees", bufs=3))
        stores = ctx.enter_context(tc.tile_pool(name="stores", bufs=2))
        psum_tr = ctx.enter_context(tc.psum_pool(name="psum_tr", bufs=3))
        psum_plain = ctx.enter_context(tc.psum_pool(name="psum_plain", bufs=2))
        psum_mx = ctx.enter_context(tc.psum_pool(name="psum_mx", bufs=3))

        ctx.enter_context(tc.manual_schedule())

        node_rows = keep.tile([P, ED], BF16)
        we_raw = keep.tile([P, HALVES, PASSES_1, PACK, BANK], BF16)
        we2_raw = keep.tile([P, PASSES_2, PACK, ED], BF16)
        x_raw = keep.tile([P, ROWS // P, K1], BF16)

        def load_we(half, c):
            nc.sync.dma_start(
                out=we_raw[:, half, c],
                in_=We[
                    c * K_PASS : (c + 1) * K_PASS, half * BANK : (half + 1) * BANK
                ].rearrange("(p t) n -> p t n", t=PACK),
            )

        def load_we2(g):
            nc.sync.dma_start(
                out=we2_raw[:, g],
                in_=We2[g * K_PASS : (g + 1) * K_PASS, :].rearrange("(p t) n -> p t n", t=PACK),
            )

        def load_x(rt):
            nc.sync.dma_start(out=x_raw[:, rt], in_=x_rows[rt * P : (rt + 1) * P, :])

        load_we(0, 0)
        load_x(0)
        nc.sync.dma_start(out=node_rows[0:NA, :], in_=a_proj)
        nc.sync.dma_start(out=node_rows[NA : NA + NB, :], in_=b_proj)
        nc.sync.dma_start(
            out=node_rows[BE1_ROW:BE2_ROW, :], in_=be1.partition_broadcast(BE2_ROW - BE1_ROW)
        )
        nc.sync.dma_start(out=node_rows[BE2_ROW:P, :], in_=be2.partition_broadcast(P - BE2_ROW))
        load_we(0, 1)
        load_x(1)
        load_we(0, 2)
        load_we(0, 3)
        load_x(2)
        load_x(3)
        for c in range(PASSES_1):
            load_we(1, c)
        load_we2(0)
        load_x(4)
        load_x(5)
        load_we2(1)
        load_x(6)
        load_x(7)

        sums_t = keep.tile([P, OUT_TILES, P], F32)
        nc.vector.memset(sums_t[:], 0.0)
        ident = keep.tile([P, P], F32)
        masks.make_identity(nc, ident[:])
        table_warmer = keep.tile([P, 1], F32)
        nc.scalar.activation(out=table_warmer[:], in_=ident[:, 0:1], func=RELU)
        ident_bf = keep.tile([P, P], BF16)
        nc.vector.tensor_copy(out=ident_bf[:], in_=ident[:])
        pick = keep.tile([P, NA, NB], BF16)
        nc.vector.tensor_tensor(
            out=pick[:],
            in0=ident[:, 0:NA].unsqueeze(2).to_broadcast([P, NA, NB]),
            in1=ident[:, NA : NA + NB].unsqueeze(1).to_broadcast([P, NA, NB]),
            op=ADD,
        )
        nc.vector.tensor_scalar_add(
            out=pick[:], in0=pick[:], scalar1=ident[:, BE1_ROW : BE1_ROW + 1]
        )
        pick_cols = pick[:].rearrange("k i j -> k (i j)")

        we_codes = keep.tile([P, PASSES_1 * ED], U32, align_bytes=64)
        we_scales = keep.tile([P, PASSES_1 * ED], U8, align_bytes=64)
        we2_codes = keep.tile([P, PASSES_2 * ED], U32, align_bytes=64)
        we2_scales = keep.tile([P, PASSES_2 * ED], U8, align_bytes=64)
        x_codes = keep.tile([P, PASSES_1 * ROWS], U32, align_bytes=64)
        x_scales = keep.tile([P, PASSES_1 * ROWS], U8, align_bytes=64)
        h_codes = keep.tile([P, PASSES_2 * ROWS], U32, align_bytes=64)
        h_scales = keep.tile([P, PASSES_2 * ROWS], U8, align_bytes=64)

        pieces = []
        for half in range(HALVES):
            for c in range(PASSES_1):
                pieces.append((we_raw[:, half, c], we_codes, we_scales, c * ED + half * BANK))
        first_we2_piece = len(pieces)
        for g in range(PASSES_2):
            for half in range(HALVES):
                cols = slice(half * BANK, (half + 1) * BANK)
                pieces.append((we2_raw[:, g, :, cols], we2_codes, we2_scales, g * ED + half * BANK))
        grouped_of = {}

        def regroup_piece(index, vector_eighths):
            raw = pieces[index][0]
            grouped = grouped_w.tile([P, BANK * PACK], BF16, align_bytes=64)
            grouped_of[index] = grouped
            if index < first_we2_piece:
                dst = grouped[:].rearrange("p (s m t) -> p m t s", s=PACK, t=PACK)
            else:
                dst = grouped[:].rearrange("p (m s t) -> p m t s", s=PACK, t=PACK)
            src = raw.rearrange("p t (m s) -> p m t s", s=PACK)
            cut = vector_eighths * P // 8
            nc.vector.tensor_copy(out=dst[:, :cut], in_=src[:, :cut])
            nc.scalar.copy(out=dst[:, cut:], in_=src[:, cut:])

        def quantise_piece(index):
            codes, scales, first_col = pieces[index][1:]
            cols = slice(first_col, first_col + BANK)
            nc.vector.quantize_mx(
                out=codes[:, cols].bitcast(FP8X4), scales=scales[:, cols], in_=grouped_of[index][:]
            )

        grouped_x_of = {}

        def transpose_x(group, pair, q):
            if (group, pair) not in grouped_x_of:
                grouped = grouped_x.tile([P, 2 * GROUP * PACK], BF16, align_bytes=64)
                grouped_x_of[group, pair] = grouped
            words = x_raw[:, group * TILES + q].bitcast(F32)
            xt = psum_tr.tile([P, 4, P], F32, tag="tr")
            for index in range(4):
                c, u = divmod(pair * 4 + index, 2)
                first = c * 2 * P
                nc.tensor.transpose(
                    xt[:, index, :], words[:, first + u : first + 2 * P : 2], ident[:]
                )
            grouped_words = grouped_x_of[group, pair][:].bitcast(F32)
            nc.scalar.copy(
                out=grouped_words.rearrange("p (c q r u) -> p q c r u", c=2, r=P, u=2)[:, q],
                in_=xt[:].rearrange("p (c u) r -> p c r u", u=2),
            )

        def x_columns(group, c, passes):
            first = (group * PASSES_1 + c) * GROUP
            return slice(first, first + passes * GROUP)

        def quantise_x(group, pair):
            cols = x_columns(group, 2 * pair, 2)
            nc.vector.quantize_mx(
                out=x_codes[:, cols].bitcast(FP8X4),
                scales=x_scales[:, cols],
                in_=grouped_x_of[group, pair][:],
            )

        def edge_terms(group, g, part):
            terms_ps = psum_plain.tile([P, SLOTS, GROUP], F32, tag="plain")
            for slot in range(SLOTS):
                first = g * K_PASS + part * SLOTS + slot
                nc.tensor.matmul(
                    terms_ps[:, slot, :],
                    lhsT=node_rows[:, first : (g + 1) * K_PASS : PACK],
                    rhs=pick_cols[:, group * GROUP : (group + 1) * GROUP],
                    start=True,
                    stop=True,
                )
            terms = terms_pool.tile([P, SLOTS, GROUP], F32)
            nc.scalar.copy(out=terms[:], in_=terms_ps[:])
            return terms

        def first_product(group, g, part):
            h_ps = psum_mx.tile([P, SLOTS, GROUP], F32, tag="mx")
            for slot in range(SLOTS):
                first_col = g * BANK + (part * SLOTS + slot) * P
                for c in range(PASSES_1):
                    w_cols = slice(c * ED + first_col, c * ED + first_col + P)
                    r_cols = x_columns(group, c, 1)
                    nc.tensor.matmul_mx(
                        out=h_ps[:, slot, :],
                        lhsT=we_codes[:, w_cols].bitcast(FP8X4),
                        lhsT_scale=we_scales[:, w_cols],
                        rhs=x_codes[:, r_cols].bitcast(FP8X4),
                        rhs_scale=x_scales[:, r_cols],
                        start=(c == 0),
                        stop=(c == PASSES_1 - 1),
                    )
            return h_ps

        def add_terms(part, h_ps, terms, sums_h):
            slots = slice(part * SLOTS, (part + 1) * SLOTS)
            nc.vector.tensor_tensor(out=sums_h[:, slots, :], in0=h_ps[:], in1=terms[:], op=ADD)

        def relu_hidden(sums_h):
            grouped = hidden.tile([P, GROUP, PACK], BF16, align_bytes=64)
            nc.vector.tensor_scalar_max(
                out=grouped[:].rearrange("p (r i) t -> p r t i", i=PACK),
                in0=sums_h[:].rearrange("p t (r i) -> p r t i", i=PACK),
                scalar1=0.0,
            )
            return grouped

        def h_columns(g, group):
            first = g * ROWS + group * GROUP
            return slice(first, first + GROUP)

        def quantise_hidden(group, g, grouped):
            cols = h_columns(g, group)
            nc.vector.quantize_mx(
                out=h_codes[:, cols].bitcast(FP8X4),
                scales=h_scales[:, cols],
                in_=grouped[:].rearrange("p r t -> p (r t)"),
            )

        be2_cols = keep.tile([P, OUT_TILES], F32)

        def transpose_be2():
            be2_ps = psum_plain.tile([P, OUT_TILES, 2], F32, tag="plain")
            for ft in range(OUT_TILES):
                nc.tensor.matmul(
                    be2_ps[:, ft, :],
                    lhsT=node_rows[:, ft * P : (ft + 1) * P],
                    rhs=ident_bf[:, BE2_ROW : BE2_ROW + 2],
                    start=True,
                    stop=True,
                )
            nc.scalar.copy(out=be2_cols[:], in_=be2_ps[:, :, 0])

        latent_of, natural_of, tree_of = {}, {}, {}

        def second_product(group, part):
            o_ps = psum_mx.tile([P, SLOTS, GROUP], F32, tag="mx")
            latent = latent_pool.tile([P, SLOTS, GROUP], F32)
            latent_of[group, part] = latent
            for slot in range(SLOTS):
                first_col = (part * SLOTS + slot) * P
                for g in range(PASSES_2):
                    f_cols = slice(g * ED + first_col, g * ED + first_col + P)
                    r_cols = h_columns(g, group)
                    nc.tensor.matmul_mx(
                        out=o_ps[:, slot, :],
                        lhsT=we2_codes[:, f_cols].bitcast(FP8X4),
                        lhsT_scale=we2_scales[:, f_cols],
                        rhs=h_codes[:, r_cols].bitcast(FP8X4),
                        rhs_scale=h_scales[:, r_cols],
                        start=(g == 0),
                        stop=(g == PASSES_2 - 1),
                    )
            for slot in range(SLOTS):
                ft = part * SLOTS + slot
                nc.scalar.activation(
                    out=latent[:, slot, :],
                    in_=o_ps[:, slot, :],
                    func=RELU,
                    bias=be2_cols[:, ft : ft + 1],
                )

        def on_gpsimd(group, part):
            return part % 2 == 0

        def out_tiles(part):
            return slice(part * SLOTS, (part + 1) * SLOTS)

        def start_tree(group, part):
            tree = trees.tile([P, SLOTS, GROUP], F32)
            tree_of[group, part] = tree

        def add_up_b_nodes(group, part):
            nc.vector.tensor_reduce(
                out=sums_t[:, out_tiles(part), group * GROUP_NA : (group + 1) * GROUP_NA],
                in_=latent_of[group, part][:].rearrange("p f (i j) -> p f i j", j=NB),
                axis=AXIS_X,
                op=ADD,
            )

        def sum_b_of(part):
            return sums_t[:, out_tiles(part), NA : NA + NB]

        def halve(engine, group, part, step, out=None):
            left = GROUP >> step
            tree = tree_of[group, part]
            source, first = (tree, GROUP - 2 * left) if step > 0 else (latent_of[group, part], 0)
            engine.tensor_tensor(
                out=tree[:, :, GROUP - left : GROUP - left // 2] if out is None else out,
                in0=source[:, :, first : first + left // 2],
                in1=source[:, :, first + left // 2 : first + left],
                op=ADD,
            )

        def add_to_sum_b(engine, group, part):
            so_far = sum_b_of(part)
            group_sum = tree_of[group, part][:, :, GROUP - 2 * NB : GROUP - NB]
            engine.tensor_tensor(out=so_far, in0=so_far, in1=group_sum, op=ADD)

        def transpose_out(group, part):
            if part == 0:
                natural = stores.tile([P, TILES, ED], F32)
                natural_of[group] = natural
            rows_ps = psum_tr.tile([P, TILES, SLOTS, P], F32, tag="tr")
            for slot in range(SLOTS):
                for q in range(TILES):
                    nc.tensor.transpose(
                        rows_ps[:, q, slot, :],
                        latent_of[group, part][:, slot, q * P : (q + 1) * P],
                        ident[:],
                    )
            last_col = (part + 1) * SLOTS * P
            nc.scalar.copy(
                out=natural_of[group][:, :, last_col - SLOTS * P : last_col],
                in_=rows_ps[:].rearrange("p q f r -> p q (f r)"),
            )
            if last_col % BANK == 0:
                cols = slice(last_col - BANK, last_col)
                nc.sync.dma_start(
                    out=latent_rows[group * GROUP : (group + 1) * GROUP, cols].rearrange(
                        "(q p) f -> p q f", p=P
                    ),
                    in_=natural_of[group][:, :, cols],
                )

        sums = keep.tile([P, ED], F32)

        def finish_sums(half):
            for quarter in range(2):
                first = half * BANK + quarter * 2 * P
                sums_ps = psum_tr.tile([P, 2, P], F32, tag="tr")
                for q in range(2):
                    nc.tensor.transpose(sums_ps[:, q, :], sums_t[:, first // P + q, :], ident[:])
                copy = nc.scalar.copy if quarter == 0 else nc.vector.tensor_copy
                copy(
                    out=sums[:, first : first + 2 * P],
                    in_=sums_ps[:].rearrange("p q f -> p (q f)"),
                )
            cols = slice(half * BANK, (half + 1) * BANK)
            nc.sync.dma_start(out=out_1[:, cols], in_=sums[0:NA, cols])
            nc.sync.dma_start(out=out_2[:, cols], in_=sums[NA : NA + NB, cols])

        units = [(g, group) for g in range(PASSES_2) for group in (0, 1)]
        units += [(g, group) for group in (2, 3) for g in range(PASSES_2)]
        beats = [(g, group, part) for g, group in units for part in range(PARTS_1)]
        outs = [(group, part) for group in range(GROUPS) for part in range(PARTS_2)]
        C_BEAT = 8

        def pieces_in(beat):
            return [index for index in range(4, len(pieces)) if beat == index - (4 if index < 6 else 5)]

        x_first = {1: (0, 2), 2: (5, 2), 3: (7, 1)}

        def x_banks_in(beat):
            return [
                (group, index // TILES, index % TILES)
                for group, (first, per_beat) in x_first.items()
                for index in range(2 * TILES)
                if beat == first + index // per_beat
            ]

        def outs_in(beat):
            if beat < C_BEAT:
                return 0
            if beat < len(beats):
                return 2 if beat > C_BEAT and beat % 3 == 2 else 1
            return 2

        regroup_piece(0, 4)
        transpose_x(0, 0, 0)
        transpose_x(0, 1, 0)
        regroup_piece(1, 6)
        quantise_piece(0)
        terms_of = {0: edge_terms(0, 0, 0)}
        transpose_x(0, 0, 1)
        regroup_piece(2, 6)
        quantise_piece(1)
        transpose_x(0, 1, 1)
        quantise_x(0, 0)
        regroup_piece(3, 6)
        quantise_piece(2)
        quantise_x(0, 1)
        quantise_piece(3)
        terms_of[1] = edge_terms(0, 0, 1)
        transpose_be2()

        h_of, sums_h_of = {}, {}
        made, summed, added = 0, 0, 0
        x_ready, pieces_ready = [], []
        beat = 0
        while added < len(outs):
            if 0 < beat <= len(beats):
                part = beats[beat - 1][2]
                add_terms(part, h_of[beat - 1], terms_of[beat - 1], sums_h_of[(beat - 1) // PARTS_1])
            for group, pair in x_ready:
                quantise_x(group, pair)
            for index in pieces_ready:
                quantise_piece(index)

            fresh = outs[summed:made]
            for_gpsimd = [item for item in fresh if on_gpsimd(*item)]
            for_vector = [item for item in fresh if not on_gpsimd(*item)]
            for group, part in for_gpsimd:
                start_tree(group, part)
                halve(nc.gpsimd, group, part, 0)
                halve(nc.gpsimd, group, part, 1)
                if group == 0:
                    halve(nc.gpsimd, group, part, 2, out=sum_b_of(part))
                else:
                    halve(nc.gpsimd, group, part, 2)
                    add_to_sum_b(nc.gpsimd, group, part)
                add_up_b_nodes(group, part)
            for group, part in for_vector:
                start_tree(group, part)
                halve(nc.vector, group, part, 0)
            unit_ended = beat % PARTS_1 == 0 and 0 < beat <= len(beats)
            if unit_ended:
                grouped_h = relu_hidden(sums_h_of[beat // PARTS_1 - 1])
            if beat + 2 < len(beats):
                g, group, part = beats[beat + 2]
                terms_of[beat + 2] = edge_terms(group, g, part)
            x_ready = []
            for group, pair, q in x_banks_in(beat):
                transpose_x(group, pair, q)
                if q == TILES - 1:
                    x_ready.append((group, pair))
            pieces_ready = pieces_in(beat)
            for index in pieces_ready:
                regroup_piece(index, 4 if index < first_we2_piece else 3)
            for group, part in for_vector:
                add_up_b_nodes(group, part)
            for group, part in for_vector:
                halve(nc.vector, group, part, 1)
            if unit_ended:
                g, group = units[beat // PARTS_1 - 1]
                quantise_hidden(group, g, grouped_h)
            for group, part in outs[added:summed]:
                if not on_gpsimd(group, part):
                    add_to_sum_b(nc.vector, group, part)
            for group, part in for_vector:
                halve(nc.vector, group, part, 2)

            for group, part in fresh:
                transpose_out(group, part)
            for group, part in outs[added:summed]:
                if group == GROUPS - 1 and part % 2 == 1:
                    finish_sums(part // 2)
            added, summed = summed, made
            for group, part in outs[made : made + outs_in(beat)]:
                if beat > len(beats) or group < GROUPS - 1:
                    second_product(group, part)
                    made += 1

            if beat < len(beats):
                g, group, part = beats[beat]
                if part == 0:
                    sums_h = before_relu.tile([P, PACK, GROUP], BF16)
                    sums_h_of[beat // PARTS_1] = sums_h
                h_of[beat] = first_product(group, g, part)
            beat += 1
